import numpy as np
import ml_dtypes


def mxq(x, axis, fmt="e4m3"):
    dtype, down = {"e4m3": (ml_dtypes.float8_e4m3fn, 7), "e5m2": (ml_dtypes.float8_e5m2, 14)}[fmt]
    v = np.moveaxis(np.asarray(x, np.float32).astype(ml_dtypes.bfloat16).astype(np.float64), axis, -1)
    blocks = v.reshape(v.shape[:-1] + (-1, 32))
    amax = np.abs(blocks).max(-1, keepdims=True)
    byte = np.maximum(np.where(amax > 0, np.frexp(amax)[1] - 1 + 127, 0) - down, 1)
    scale = np.exp2(byte - 127.0)
    codes = (blocks / scale).astype(np.float32).astype(dtype).astype(np.float64)
    return np.moveaxis((codes * scale).reshape(v.shape), -1, axis)


WIDE = False


def mx_kscale(k):
    if not WIDE:
        return np.ones(k)
    levels = np.array([10, -10, 5, -5, 0])
    a = np.random.permutation(np.resize(levels, k // 512 * 4)).reshape(k // 512, 4)
    idx = np.arange(k)
    return np.exp2(a[idx // 512, idx % 128 // 32])


BF16 = ml_dtypes.bfloat16


def bf(x):
    return np.asarray(x, np.float32).astype(BF16)


def f64(x):
    return np.asarray(x).astype(np.float64)


E2M1 = np.array([0.0, 0.5, 1.0, 1.5, 2.0, 3.0, 4.0, 6.0, -0.0, -0.5, -1.0, -1.5, -2.0, -3.0, -4.0, -6.0])


def pack_weight(w, fmt):
    k, n = w.shape
    w = f64(bf(w)).reshape(k // 32, 32, n)
    amax = np.abs(w).max(1)
    if fmt == "e4m3":
        byte = np.frexp(amax)[1] - 1 + 127 - 7
    else:
        mant, ex = np.frexp(amax / 6.0)
        byte = np.where(mant > 0.5, ex, ex - 1) + 127
    byte = np.clip(np.where(amax > 0, byte, 1), 1, 254)
    scaled = (w * np.exp2(127.0 - byte)[:, None, :]).reshape(k, n).astype(np.float32)
    by_word = np.ascontiguousarray(scaled.reshape(k // 512, 128, 4, n).transpose(0, 1, 3, 2))
    if fmt == "e4m3":
        words = by_word.astype(ml_dtypes.float8_e4m3fn).view(np.uint8)
    else:
        c = by_word.astype(ml_dtypes.float4_e2m1fn).view(np.uint8) & 0xF
        words = c[..., 0::2] | (c[..., 1::2] << 4)
    return np.ascontiguousarray(words), np.ascontiguousarray(byte.astype(np.uint8).reshape(k // 512, 16, n))


def unpack_weight(words, scales, fmt):
    g, p, n, _ = words.shape
    if fmt == "e4m3":
        vals = np.ascontiguousarray(words).view(ml_dtypes.float8_e4m3fn).astype(np.float64)
    else:
        nib = np.empty((g, p, n, 4), np.uint8)
        nib[..., 0::2] = words & 0xF
        nib[..., 1::2] = words >> 4
        vals = E2M1[nib]
    vals = vals * np.repeat(np.exp2(scales.astype(np.float64) - 127.0), 8, axis=1)[..., None]
    return vals.transpose(0, 1, 3, 2).reshape(g * 512, n)


B, S, D = 16, 1024, 128
EPS = 1e-5
FMT = "e4m3"


def hardswish(v):
    return v * np.clip(v + 3.0, 0.0, 6.0) / 6.0


def setup_inputs():
    s = mx_kscale(S)
    x = bf(np.random.standard_normal((B, S, D)))
    ln_w = bf((1.0 + 0.1 * np.random.standard_normal((S, D))) * s[:, None])
    ln_b = bf(0.1 * np.random.standard_normal((S, D)) * s[:, None])
    w1 = np.random.standard_normal((S, S)) * 0.05 / s[None, :]
    w2 = np.random.standard_normal((S, S)) * 0.06
    mask = np.tril(np.ones((S, S)))
    W1_words, W1_scales = pack_weight(np.ascontiguousarray((w1 * mask).T), FMT)
    W2_words, W2_scales = pack_weight(np.ascontiguousarray((w2 * mask).T), FMT)
    return {"x": x,
            "ln_w": ln_w,
            "ln_b": ln_b,
            "W1_words": W1_words, "W1_scales": W1_scales,
            "W2_words": W2_words, "W2_scales": W2_scales}


def reference(x, ln_w, ln_b, W1_words, W1_scales, W2_words, W2_scales):
    x = f64(x)
    mu = np.mean(x, axis=(-2, -1), keepdims=True)
    var = np.mean(np.square(x - mu), axis=(-2, -1), keepdims=True)
    h = (x - mu) * (1.0 / np.sqrt(var + EPS)) * f64(ln_w) + f64(ln_b)
    a1 = unpack_weight(W1_words, W1_scales, FMT).T
    a2 = unpack_weight(W2_words, W2_scales, FMT).T
    u = hardswish(a1 @ mxq(h, 1, "e4m3"))
    v = a2 @ mxq(u, 1, "e4m3")
    return x + v

@@ -1,0 +1,310 @@
+from contextlib import ExitStack
+
+import concourse.mybir as mybir
+from concourse.masks import make_identity
+
+F32 = mybir.dt.float32
+BF16 = mybir.dt.bfloat16
+U32 = mybir.dt.uint32
+U8 = mybir.dt.uint8
+I32 = mybir.dt.int32
+FP8X4 = mybir.dt.float8_e4m3fn_x4
+ALU = mybir.AluOpType
+ACT = mybir.ActivationFunctionType
+
+B, S, D = 16, 1024, 128
+P = 128
+EPS = 1e-5
+NTOT = S * D
+FLOPS = 2 * 2 * S * S * B * D
+
+MANUAL = False
+GROUPS = [[0, 1], [2, 3], [4, 5, 6, 7], [8, 9, 10, 11], [12, 13, 14, 15]]
+
+
+def tile_timemixing_kernel(tc, x, ln_w, ln_b, W1_words, W1_scales, W2_words, W2_scales, out):
+    nc = tc.nc
+    with ExitStack() as ctx:
+        ctx.enter_context(nc.allow_non_contiguous_dma(reason="rows of 256 B to 2 KiB"))
+        keep = ctx.enter_context(tc.tile_pool(name="keep", bufs=1))
+        small = ctx.enter_context(tc.tile_pool(name="small", bufs=2))
+        work = ctx.enter_context(tc.tile_pool(name="work", bufs=3))
+        rpool = ctx.enter_context(tc.tile_pool(name="rpool", bufs=4))
+        upool = ctx.enter_context(tc.tile_pool(name="upool", bufs=2))
+        opool = ctx.enter_context(tc.tile_pool(name="opool", bufs=4))
+        psA = ctx.enter_context(tc.psum_pool(name="psA", bufs=4))
+        psT = ctx.enter_context(tc.psum_pool(name="psT", bufs=1))
+        psV = ctx.enter_context(tc.psum_pool(name="psV", bufs=2))
+        psS = ctx.enter_context(tc.psum_pool(name="psS", bufs=1))
+        if MANUAL:
+            ctx.enter_context(tc.manual_schedule())
+
+        wpl = keep.tile([P, 4, S], U8, align_bytes=64, name="wpl")
+        nc.vector.memset(wpl[:].bitcast(I32), 0)
+        ones_f = keep.tile([P, P], F32, name="ones_f")
+        nc.vector.memset(ones_f[:], 1.0)
+        ones_b = keep.tile([P, 2], BF16, name="ones_b")
+        nc.vector.memset(ones_b[:], 1.0)
+        ident = keep.tile([P, P], BF16, name="ident")
+        make_identity(nc, ident[:])
+        warm = keep.tile([P, 1], F32, name="warm")
+        nc.scalar.activation(out=warm[:], in_=ones_f[:, 0:1], func=ACT.Sqrt)
+
+        sq_all = keep.tile([P, B], F32, name="sq_all")
+        mean_all = keep.tile([P, B], F32, name="mean_all")
+        rstd_all = keep.tile([P, B], F32, name="rstd_all")
+
+        xq = [keep.tile([P, S], BF16, name="xq%d" % b) for b in range(B)]
+        xn = [keep.tile([P, 4, 8, D], BF16, name="xn%d" % q) for q in range(4)]
+        lnw = keep.tile([P, S], BF16, name="lnw")
+        lnb = keep.tile([P, S], BF16, name="lnb")
+        wc = [keep.tile([P, 2, S], U32, align_bytes=64, name="wc%d" % w) for w in range(2)]
+
+        def load_xq(b):
+            nc.sync.dma_start(
+                out=xq[b][:].rearrange("p (g c) -> p g c", g=2),
+                in_=x[b].rearrange("(g p j) d -> p g (j d)", g=2, p=P, j=4),
+            )
+
+        def load_xn(q):
+            nc.sync.dma_start(
+                out=xn[q][:].rearrange("c b m d -> c (b m) d"),
+                in_=x[4 * q : 4 * q + 4].rearrange("b (m c) d -> c (b m) d", c=P),
+            )
+
+        def load_w(w, words, scales):
+            by_row = scales.rearrange("g (q r) n -> r q g n", r=4)
+            for r in range(4):
+                nc.sync.dma_start(
+                    out=wpl[r:P:32, 2 * w : 2 * w + 2, :].bitcast(I32),
+                    in_=by_row[r].bitcast(I32),
+                )
+            nc.sync.dma_start(
+                out=wc[w][:, 0, :].bitcast(I32),
+                in_=words[0].rearrange("p n t -> p (n t)").bitcast(I32),
+            )
+            nc.sync.dma_start(
+                out=wc[w][:, 1, 512:S].bitcast(I32),
+                in_=words[1].rearrange("p n t -> p (n t)").bitcast(I32)[:, 512:S],
+            )
+
+        for b in range(4):
+            load_xq(b)
+        for dst, src in ((lnw, ln_w), (lnb, ln_b)):
+            nc.sync.dma_start(
+                out=dst[:].rearrange("p (g c) -> p g c", g=2),
+                in_=src.rearrange("(g p j) d -> p g (j d)", g=2, p=P, j=4),
+            )
+        load_w(0, W1_words, W1_scales)
+        for b in range(4, 8):
+            load_xq(b)
+        load_w(1, W2_words, W2_scales)
+        for b in range(8, 12):
+            load_xq(b)
+        load_xn(0)
+        for b in range(12, 16):
+            load_xq(b)
+        for q in range(1, 4):
+            load_xn(q)
+
+        lnw_g = keep.tile([P, 2, D, 4], BF16, name="lnw_g")
+        lnb_g = keep.tile([P, 2, D, 4], BF16, name="lnb_g")
+        nc.vector.tensor_copy(out=lnw_g[:], in_=lnw[:].rearrange("p (g j d) -> p g d j", g=2, j=4))
+        nc.vector.tensor_copy(out=lnb_g[:], in_=lnb[:].rearrange("p (g j d) -> p g d j", g=2, j=4))
+
+        hc = [keep.tile([P, 2 * D], U32, align_bytes=64, name="hc%d" % b) for b in range(B)]
+        hp = [keep.tile([P, 2 * D], U8, align_bytes=64, name="hp%d" % b) for b in range(B)]
+
+        st_tiles = {}
+        hg_tiles = {}
+        acc_tiles = {}
+        r_tiles = {}
+        u_tiles = {}
+        v_tiles = {}
+
+        def group_of(b):
+            return [k for k in range(len(GROUPS)) if b in GROUPS[k]][0]
+
+        def square(b):
+            k = group_of(b)
+            grp = GROUPS[k]
+            if b == grp[0]:
+                st = psS.tile([P, 32], F32, name="st")
+                st_tiles[k] = st
+            st = st_tiles[k]
+            junk = work.tile([P, S], BF16, name="junk")
+            nc.scalar.activation(out=junk[:], in_=xq[b][:], func=ACT.Square, accum_out=sq_all[:, b : b + 1])
+            bl = b - grp[0]
+            for c in range(8):
+                nc.tensor.matmul(
+                    out=st[:, 2 * bl : 2 * bl + 2],
+                    lhsT=xq[b][:, P * c : P * c + P],
+                    rhs=ones_b[:],
+                    start=(c == 0),
+                    stop=(c == 7),
+                )
+
+        def chain(k):
+            grp = GROUPS[k]
+            n = len(grp)
+            b0 = grp[0]
+            st = st_tiles[k]
+            cs_sb = small.tile([P, 4], F32, name="cs_sb")
+            nc.vector.tensor_copy(out=cs_sb[:, 0:n], in_=st[:, 0 : 2 * n : 2])
+            nc.tensor.matmul(out=st[:, 16 : 16 + n], lhsT=ones_f[:], rhs=cs_sb[:, 0:n], start=True, stop=True)
+            nc.tensor.matmul(out=st[:, 24 : 24 + n], lhsT=ones_f[:], rhs=sq_all[:, b0 : b0 + n], start=True, stop=True)
+            mean = mean_all[:, b0 : b0 + n]
+            nc.vector.tensor_scalar(out=mean, in0=st[:, 16 : 16 + n], scalar1=1.0 / NTOT, scalar2=None, op0=ALU.mult)
+            ve = small.tile([P, 4], F32, name="ve")
+            nc.vector.tensor_scalar(
+                out=ve[:, 0:n], in0=st[:, 24 : 24 + n], scalar1=1.0 / NTOT, scalar2=EPS, op0=ALU.mult, op1=ALU.add
+            )
+            msq = small.tile([P, 4], F32, name="msq")
+            nc.vector.tensor_tensor(out=msq[:, 0:n], in0=mean, in1=mean, op=ALU.mult)
+            nc.vector.tensor_tensor(out=ve[:, 0:n], in0=ve[:, 0:n], in1=msq[:, 0:n], op=ALU.subtract)
+            std = small.tile([P, 4], F32, name="std")
+            nc.scalar.activation(out=std[:, 0:n], in_=ve[:, 0:n], func=ACT.Sqrt)
+            nc.vector.reciprocal(out=rstd_all[:, b0 : b0 + n], in_=std[:, 0:n])
+
+        def ln(b):
+            t = work.tile([P, 2, D, 4], F32, name="t")
+            for g in range(2):
+                nc.vector.scalar_tensor_tensor(
+                    out=t[:, g],
+                    in0=xq[b][:, 512 * g : 512 * g + 512].rearrange("p (j d) -> p d j", j=4),
+                    scalar=mean_all[:, b : b + 1],
+                    in1=lnw_g[:, g],
+                    op0=ALU.subtract,
+                    op1=ALU.mult,
+                )
+            hg = work.tile([P, 2, D, 4], BF16, align_bytes=64, name="hg")
+            nc.vector.scalar_tensor_tensor(
+                out=hg[:].rearrange("p g d j -> p (g d j)"),
+                in0=t[:].rearrange("p g d j -> p (g d j)"),
+                scalar=rstd_all[:, b : b + 1],
+                in1=lnb_g[:].rearrange("p g d j -> p (g d j)"),
+                op0=ALU.mult,
+                op1=ALU.add,
+            )
+            hg_tiles[b] = hg
+
+        def quant_h(b):
+            nc.vector.quantize_mx(
+                out=hc[b][:].bitcast(FP8X4),
+                scales=hp[b][:],
+                in_=hg_tiles[b][:].rearrange("p g d j -> p (g d j)"),
+            )
+
+        def mm1(b):
+            for tcn in range(2):
+                acc = psA.tile([P, 512], F32, name="acc")
+                for g in range(tcn + 1):
+                    nc.tensor.matmul_mx(
+                        out=acc[:],
+                        lhsT=hc[b][:, D * g : D * g + D].bitcast(FP8X4),
+                        lhsT_scale=hp[b][:, D * g : D * g + D],
+                        rhs=wc[0][:, g, 512 * tcn : 512 * tcn + 512].bitcast(FP8X4),
+                        rhs_scale=wpl[:, g, 512 * tcn : 512 * tcn + 512],
+                        start=(g == 0),
+                        stop=(g == tcn),
+                    )
+                r = rpool.tile([P, 512], F32, name="r")
+                nc.scalar.activation(out=r[:], in_=acc[:], func=ACT.Relu, bias=0.5, scale=1.0 / 6.0)
+                acc_tiles[(b, tcn)] = acc
+                r_tiles[(b, tcn)] = r
+
+        def hs2(b):
+            uT = work.tile([P, S], BF16, name="uT")
+            for tcn in range(2):
+                nc.vector.scalar_tensor_tensor(
+                    out=uT[:, 512 * tcn : 512 * tcn + 512],
+                    in0=r_tiles[(b, tcn)][:],
+                    scalar=1.0,
+                    in1=acc_tiles[(b, tcn)][:],
+                    op0=ALU.min,
+                    op1=ALU.mult,
+                )
+            q, bl = divmod(b, 4)
+            if bl == 0:
+                ug = upool.tile([P, 2, 4, D, 4], BF16, align_bytes=64, name="ug")
+                u_tiles[q] = ug
+            ug = u_tiles[q]
+            tp = psT.tile([P, 2, 4, D], BF16, name="tp")
+            for g in range(2):
+                for j in range(4):
+                    nc.tensor.transpose(
+                        out=tp[:, g, j, :],
+                        in_=uT[:, 512 * g + j : 512 * (g + 1) : 4],
+                        identity=ident[:],
+                    )
+            nc.scalar.copy(out=ug[:, :, bl, :, :], in_=tp[:].rearrange("p g j d -> p g d j"))
+
+        def quant_u(q):
+            uc = upool.tile([P, 2, 512], U32, align_bytes=64, name="uc")
+            up = upool.tile([P, 2, 512], U8, align_bytes=64, name="up")
+            for g in range(2):
+                nc.vector.quantize_mx(
+                    out=uc[:, g, :].bitcast(FP8X4),
+                    scales=up[:, g, :],
+                    in_=u_tiles[q][:, g].rearrange("p b d j -> p (b d j)"),
+                )
+            u_tiles[(q, "c")] = (uc, up)
+
+        def mm2(k):
+            q, mp = divmod(k, 4)
+            uc, up = u_tiles[(q, "c")]
+            for m in (2 * mp, 2 * mp + 1):
+                vps = psV.tile([P, 512], F32, name="vps")
+                top = m // 4
+                for g in range(top + 1):
+                    nc.tensor.matmul_mx(
+                        out=vps[:],
+                        lhsT=wc[1][:, g, P * m : P * m + P].bitcast(FP8X4),
+                        lhsT_scale=wpl[:, 2 + g, P * m : P * m + P],
+                        rhs=uc[:, g, :].bitcast(FP8X4),
+                        rhs_scale=up[:, g, :],
+                        start=(g == 0),
+                        stop=(g == top),
+                    )
+                v_tiles[(q, m)] = vps
+
+        def resid(k):
+            q, mp = divmod(k, 4)
+            for m in (2 * mp, 2 * mp + 1):
+                ot = opool.tile([P, 4, D], F32, name="ot")
+                nc.vector.tensor_tensor(
+                    out=ot[:],
+                    in0=v_tiles[(q, m)][:].rearrange("p (b d) -> p b d", b=4),
+                    in1=xn[q][:, :, m, :],
+                    op=ALU.add,
+                )
+                nc.sync.dma_start(
+                    out=out[4 * q : 4 * q + 4, P * m : P * m + P, :].rearrange("b c d -> c b d"),
+                    in_=ot[:],
+                )
+
+        for b in range(4):
+            square(b)
+            if b == 1:
+                chain(0)
+            if b == 3:
+                chain(1)
+        for s in range(-2, 22):
+            if s >= 1 and (s + 3) % 4 == 0 and (s + 3) // 4 <= 3:
+                chain((s + 3) // 4 + 1)
+            for b in range(4, B):
+                if max(-2, b - 7) == s:
+                    square(b)
+            if s + 2 < B:
+                ln(s + 2)
+            if 0 <= s + 1 < B:
+                quant_h(s + 1)
+                mm1(s + 1)
+            if 0 <= s < B:
+                hs2(s)
+            if s >= 5 and (s - 5) % 4 == 0 and (s - 5) // 4 <= 3:
+                quant_u((s - 5) // 4)
+            if 0 <= s - 6 < 16:
+                resid(s - 6)
+            if 0 <= s - 5 < 16:
+                mm2(s - 5)

@@ -19,7 +19,15 @@ NTOT = S * D
 FLOPS = 2 * 2 * S * S * B * D
 
 MANUAL = False
-GROUPS = [[0, 1], [2, 3], [4, 5, 6, 7], [8, 9, 10, 11], [12, 13, 14, 15]]
+GB = [3,6,8,10,12,13,14]
+GROUPS = [[0], [1], [2, 3], [4, 5, 6, 7], [8, 9, 10, 11], [12, 13, 14, 15]]
+RES_AT = {5: (1, 1), 6: (1, 1), 7: (1, 1), 8: (1, 1), 9: (1, 1), 10: (1, 1), 11: (1, 1), 12: (1, 1), 13: (2, 0), 14: (2, 0), 15: (2, 0), 16: (2, 0), 17: (8, 0)}
+SQ = {-3: (4, 5, 6), -2: (7,), -1: (8, 9), 0: (10, 11), 1: (12, 13), 2: (14, 15)}
+CA = {3: -2, 4: 0, 5: 2}
+CS = {2: -3, 3: -1, 4: 1, 5: 3}
+CC = {1: -3, 2: -2, 3: -1, 4: 1, 5: 3}
+GR = {-2: (3,), -1: (6,), 1: (8, 10), 3: (12, 13, 14)}
+LATE = 16
 
 
 def tile_timemixing_kernel(tc, x, ln_w, ln_b, W1_words, W1_scales, W2_words, W2_scales, out):
@@ -27,15 +35,16 @@ def tile_timemixing_kernel(tc, x, ln_w, ln_b, W1_words, W1_scales, W2_words, W2_
     with ExitStack() as ctx:
         ctx.enter_context(nc.allow_non_contiguous_dma(reason="rows of 256 B to 2 KiB"))
         keep = ctx.enter_context(tc.tile_pool(name="keep", bufs=1))
-        small = ctx.enter_context(tc.tile_pool(name="small", bufs=2))
+        small = ctx.enter_context(tc.tile_pool(name="small", bufs=3))
         work = ctx.enter_context(tc.tile_pool(name="work", bufs=3))
+        gpool = ctx.enter_context(tc.tile_pool(name="gpool", bufs=2))
         rpool = ctx.enter_context(tc.tile_pool(name="rpool", bufs=4))
         upool = ctx.enter_context(tc.tile_pool(name="upool", bufs=2))
-        opool = ctx.enter_context(tc.tile_pool(name="opool", bufs=4))
-        psA = ctx.enter_context(tc.psum_pool(name="psA", bufs=4))
+        opool = ctx.enter_context(tc.tile_pool(name="opool", bufs=8))
+        psL = ctx.enter_context(tc.psum_pool(name="psL", bufs=1))
+        psA = ctx.enter_context(tc.psum_pool(name="psA", bufs=3))
         psT = ctx.enter_context(tc.psum_pool(name="psT", bufs=1))
         psV = ctx.enter_context(tc.psum_pool(name="psV", bufs=2))
-        psS = ctx.enter_context(tc.psum_pool(name="psS", bufs=1))
         if MANUAL:
             ctx.enter_context(tc.manual_schedule())
 
@@ -50,8 +59,8 @@ def tile_timemixing_kernel(tc, x, ln_w, ln_b, W1_words, W1_scales, W2_words, W2_
         warm = keep.tile([P, 1], F32, name="warm")
         nc.scalar.activation(out=warm[:], in_=ones_f[:, 0:1], func=ACT.Sqrt)
 
-        sq_all = keep.tile([P, B], F32, name="sq_all")
-        mean_all = keep.tile([P, B], F32, name="mean_all")
+        stat = [keep.tile([P, 2 * len(GROUPS[k])], F32, name="stat%d" % k) for k in range(len(GROUPS))]
+        negmean_all = keep.tile([P, B], F32, name="negmean_all")
         rstd_all = keep.tile([P, B], F32, name="rstd_all")
 
         xq = [keep.tile([P, S], BF16, name="xq%d" % b) for b in range(B)]
@@ -88,34 +97,44 @@ def tile_timemixing_kernel(tc, x, ln_w, ln_b, W1_words, W1_scales, W2_words, W2_
                 in_=words[1].rearrange("p n t -> p (n t)").bitcast(I32)[:, 512:S],
             )
 
-        for b in range(4):
-            load_xq(b)
+        load_xq(0)
+        load_xq(1)
         for dst, src in ((lnw, ln_w), (lnb, ln_b)):
             nc.sync.dma_start(
                 out=dst[:].rearrange("p (g c) -> p g c", g=2),
                 in_=src.rearrange("(g p j) d -> p g (j d)", g=2, p=P, j=4),
             )
+        load_xq(2)
+        load_xq(3)
         load_w(0, W1_words, W1_scales)
-        for b in range(4, 8):
+        for b in range(4, B):
             load_xq(b)
         load_w(1, W2_words, W2_scales)
-        for b in range(8, 12):
-            load_xq(b)
-        load_xn(0)
-        for b in range(12, 16):
-            load_xq(b)
-        for q in range(1, 4):
+        for q in range(4):
             load_xn(q)
 
         lnw_g = keep.tile([P, 2, D, 4], BF16, name="lnw_g")
         lnb_g = keep.tile([P, 2, D, 4], BF16, name="lnb_g")
-        nc.vector.tensor_copy(out=lnw_g[:], in_=lnw[:].rearrange("p (g j d) -> p g d j", g=2, j=4))
-        nc.vector.tensor_copy(out=lnb_g[:], in_=lnb[:].rearrange("p (g j d) -> p g d j", g=2, j=4))
+        lnw_ps = psL.tile([P, 2, D, 4], BF16, name="lnw_ps")
+        lnb_ps = psL.tile([P, 2, D, 4], BF16, name="lnb_ps")
+
+        def place_ln():
+            for nat, grouped, bank in ((lnw, lnw_g, lnw_ps), (lnb, lnb_g, lnb_ps)):
+                nc.vector.tensor_copy(out=grouped[:], in_=nat[:].rearrange("p (g j d) -> p g d j", g=2, j=4))
+                for g in range(2):
+                    nc.tensor.matmul(
+                        out=bank[:, g].rearrange("p d j -> p (d j)"),
+                        lhsT=ident[:],
+                        rhs=grouped[:, g].rearrange("p d j -> p (d j)"),
+                        start=True,
+                        stop=True,
+                    )
 
         hc = [keep.tile([P, 2 * D], U32, align_bytes=64, name="hc%d" % b) for b in range(B)]
         hp = [keep.tile([P, 2 * D], U8, align_bytes=64, name="hp%d" % b) for b in range(B)]
 
         st_tiles = {}
+        ch_tiles = {}
         hg_tiles = {}
         acc_tiles = {}
         r_tiles = {}
@@ -129,12 +148,12 @@ def tile_timemixing_kernel(tc, x, ln_w, ln_b, W1_words, W1_scales, W2_words, W2_
             k = group_of(b)
             grp = GROUPS[k]
             if b == grp[0]:
-                st = psS.tile([P, 32], F32, name="st")
-                st_tiles[k] = st
+                st_new = psV.tile([P, 512], F32, name="vps")
+                st_tiles[k] = st_new
             st = st_tiles[k]
-            junk = work.tile([P, S], BF16, name="junk")
-            nc.scalar.activation(out=junk[:], in_=xq[b][:], func=ACT.Square, accum_out=sq_all[:, b : b + 1])
             bl = b - grp[0]
+            junk = work.tile([P, S], BF16, name="junk")
+            nc.scalar.activation(out=junk[:], in_=xq[b][:], func=ACT.Square, accum_out=stat[k][:, bl : bl + 1])
             for c in range(8):
                 nc.tensor.matmul(
                     out=st[:, 2 * bl : 2 * bl + 2],
@@ -144,27 +163,39 @@ def tile_timemixing_kernel(tc, x, ln_w, ln_b, W1_words, W1_scales, W2_words, W2_
                     stop=(c == 7),
                 )
 
-        def chain(k):
+        def chain_a(k):
+            n = len(GROUPS[k])
+            st = st_tiles[k]
+            nc.scalar.copy(out=stat[k][:, n : 2 * n], in_=st[:, 0 : 2 * n : 2])
+            nc.tensor.matmul(out=st[:, 16 : 16 + 2 * n], lhsT=ones_f[:], rhs=stat[k][:], start=True, stop=True)
+
+        def chain_s(k):
             grp = GROUPS[k]
             n = len(grp)
             b0 = grp[0]
             st = st_tiles[k]
-            cs_sb = small.tile([P, 4], F32, name="cs_sb")
-            nc.vector.tensor_copy(out=cs_sb[:, 0:n], in_=st[:, 0 : 2 * n : 2])
-            nc.tensor.matmul(out=st[:, 16 : 16 + n], lhsT=ones_f[:], rhs=cs_sb[:, 0:n], start=True, stop=True)
-            nc.tensor.matmul(out=st[:, 24 : 24 + n], lhsT=ones_f[:], rhs=sq_all[:, b0 : b0 + n], start=True, stop=True)
-            mean = mean_all[:, b0 : b0 + n]
-            nc.vector.tensor_scalar(out=mean, in0=st[:, 16 : 16 + n], scalar1=1.0 / NTOT, scalar2=None, op0=ALU.mult)
-            ve = small.tile([P, 4], F32, name="ve")
-            nc.vector.tensor_scalar(
-                out=ve[:, 0:n], in0=st[:, 24 : 24 + n], scalar1=1.0 / NTOT, scalar2=EPS, op0=ALU.mult, op1=ALU.add
-            )
+            sums = st[:, 16 + n : 16 + 2 * n]
+            nc.scalar.activation(out=negmean_all[:, b0 : b0 + n], in_=sums, func=ACT.Copy, scale=-1.0 / NTOT)
             msq = small.tile([P, 4], F32, name="msq")
-            nc.vector.tensor_tensor(out=msq[:, 0:n], in0=mean, in1=mean, op=ALU.mult)
-            nc.vector.tensor_tensor(out=ve[:, 0:n], in0=ve[:, 0:n], in1=msq[:, 0:n], op=ALU.subtract)
+            nc.scalar.activation(out=msq[:, 0:n], in_=sums, func=ACT.Square, scale=1.0 / NTOT)
+            shift = small.tile([P, 4], F32, name="shift")
+            nc.scalar.activation(out=shift[:, 0:n], in_=msq[:, 0:n], func=ACT.Identity, scale=-1.0, bias=EPS)
             std = small.tile([P, 4], F32, name="std")
-            nc.scalar.activation(out=std[:, 0:n], in_=ve[:, 0:n], func=ACT.Sqrt)
-            nc.vector.reciprocal(out=rstd_all[:, b0 : b0 + n], in_=std[:, 0:n])
+            for i in range(n):
+                nc.scalar.activation(
+                    out=std[:, i : i + 1],
+                    in_=st[:, 16 + i : 17 + i],
+                    func=ACT.Sqrt,
+                    scale=1.0 / NTOT,
+                    bias=shift[:, i : i + 1],
+                )
+            ch_tiles[k] = std
+
+        def chain_c(k):
+            grp = GROUPS[k]
+            n = len(grp)
+            b0 = grp[0]
+            nc.vector.reciprocal(out=rstd_all[:, b0 : b0 + n], in_=ch_tiles[k][:, 0:n])
 
         def ln(b):
             t = work.tile([P, 2, D, 4], F32, name="t")
@@ -172,9 +203,9 @@ def tile_timemixing_kernel(tc, x, ln_w, ln_b, W1_words, W1_scales, W2_words, W2_
                 nc.vector.scalar_tensor_tensor(
                     out=t[:, g],
                     in0=xq[b][:, 512 * g : 512 * g + 512].rearrange("p (j d) -> p d j", j=4),
-                    scalar=mean_all[:, b : b + 1],
-                    in1=lnw_g[:, g],
-                    op0=ALU.subtract,
+                    scalar=negmean_all[:, b : b + 1],
+                    in1=lnw_ps[:, g],
+                    op0=ALU.add,
                     op1=ALU.mult,
                 )
             hg = work.tile([P, 2, D, 4], BF16, align_bytes=64, name="hg")
@@ -182,11 +213,27 @@ def tile_timemixing_kernel(tc, x, ln_w, ln_b, W1_words, W1_scales, W2_words, W2_
                 out=hg[:].rearrange("p g d j -> p (g d j)"),
                 in0=t[:].rearrange("p g d j -> p (g d j)"),
                 scalar=rstd_all[:, b : b + 1],
-                in1=lnb_g[:].rearrange("p g d j -> p (g d j)"),
+                in1=lnb_ps[:].rearrange("p g d j -> p (g d j)"),
                 op0=ALU.mult,
                 op1=ALU.add,
             )
             hg_tiles[b] = hg
+
+        def g_route(b):
+            xg = gpool.tile([P, 2, D, 4], F32, name="xg")
+            hgg = keep.tile([P, 2, D, 4], BF16, align_bytes=64, name="hgg%d" % b)
+            for g in range(2):
+                nc.gpsimd.tensor_scalar(
+                    out=xg[:, g],
+                    in0=xq[b][:, 512 * g : 512 * g + 512].rearrange("p (j d) -> p d j", j=4),
+                    scalar1=negmean_all[:, b : b + 1],
+                    scalar2=rstd_all[:, b : b + 1],
+                    op0=ALU.add,
+                    op1=ALU.mult,
+                )
+                nc.gpsimd.tensor_tensor(out=xg[:, g], in0=xg[:, g], in1=lnw_g[:, g], op=ALU.mult)
+                nc.gpsimd.tensor_tensor(out=hgg[:, g], in0=xg[:, g], in1=lnb_g[:, g], op=ALU.add)
+            hg_tiles[b] = hgg
 
         def quant_h(b):
             nc.vector.quantize_mx(
@@ -208,103 +255,150 @@ def tile_timemixing_kernel(tc, x, ln_w, ln_b, W1_words, W1_scales, W2_words, W2_
                         start=(g == 0),
                         stop=(g == tcn),
                     )
-                r = rpool.tile([P, 512], F32, name="r")
-                nc.scalar.activation(out=r[:], in_=acc[:], func=ACT.Relu, bias=0.5, scale=1.0 / 6.0)
+                r = rpool.tile([P, 4, P], F32, name="r")
+                nc.scalar.activation(
+                    out=r[:], in_=acc[:].rearrange("p (q j) -> p j q", j=4), func=ACT.Relu, bias=0.5, scale=1.0 / 6.0
+                )
                 acc_tiles[(b, tcn)] = acc
                 r_tiles[(b, tcn)] = r
 
         def hs2(b):
-            uT = work.tile([P, S], BF16, name="uT")
+            uT = work.tile([P, 2, 4, P], BF16, name="uT")
             for tcn in range(2):
                 nc.vector.scalar_tensor_tensor(
-                    out=uT[:, 512 * tcn : 512 * tcn + 512],
+                    out=uT[:, tcn],
                     in0=r_tiles[(b, tcn)][:],
                     scalar=1.0,
-                    in1=acc_tiles[(b, tcn)][:],
+                    in1=acc_tiles[(b, tcn)][:].rearrange("p (q j) -> p j q", j=4),
                     op0=ALU.min,
                     op1=ALU.mult,
                 )
+            u_tiles[("T", b)] = uT
+
+        def transp(b):
+            uT = u_tiles[("T", b)]
             q, bl = divmod(b, 4)
             if bl == 0:
-                ug = upool.tile([P, 2, 4, D, 4], BF16, align_bytes=64, name="ug")
-                u_tiles[q] = ug
+                ug_new = upool.tile([P, 2, 4, D, 4], BF16, align_bytes=64, name="ug")
+                u_tiles[q] = ug_new
             ug = u_tiles[q]
             tp = psT.tile([P, 2, 4, D], BF16, name="tp")
             for g in range(2):
                 for j in range(4):
-                    nc.tensor.transpose(
-                        out=tp[:, g, j, :],
-                        in_=uT[:, 512 * g + j : 512 * (g + 1) : 4],
-                        identity=ident[:],
-                    )
-            nc.scalar.copy(out=ug[:, :, bl, :, :], in_=tp[:].rearrange("p g j d -> p g d j"))
-
-        def quant_u(q):
-            uc = upool.tile([P, 2, 512], U32, align_bytes=64, name="uc")
-            up = upool.tile([P, 2, 512], U8, align_bytes=64, name="up")
+                    nc.tensor.transpose(out=tp[:, g, j, :], in_=uT[:, g, j, :], identity=ident[:])
             for g in range(2):
-                nc.vector.quantize_mx(
-                    out=uc[:, g, :].bitcast(FP8X4),
-                    scales=up[:, g, :],
-                    in_=u_tiles[q][:, g].rearrange("p b d j -> p (b d j)"),
-                )
-            u_tiles[(q, "c")] = (uc, up)
+                nc.scalar.copy(out=ug[:, g, bl, :, :], in_=tp[:, g].rearrange("p j d -> p d j"))
 
-        def mm2(k):
-            q, mp = divmod(k, 4)
+        def quant_u(q, g):
+            if g == 0:
+                uc_new = upool.tile([P, 2, 512], U32, align_bytes=64, name="uc")
+                up_new = upool.tile([P, 2, 512], U8, align_bytes=64, name="up")
+                u_tiles[(q, "c")] = (uc_new, up_new)
             uc, up = u_tiles[(q, "c")]
-            for m in (2 * mp, 2 * mp + 1):
+            nc.vector.quantize_mx(
+                out=uc[:, g, :].bitcast(FP8X4),
+                scales=up[:, g, :],
+                in_=u_tiles[q][:, g].rearrange("p b d j -> p (b d j)"),
+            )
+
+        def mm2(u):
+            q, m = divmod(u, 8)
+            uc, up = u_tiles[(q, "c")]
+            turn = (u - LATE) % 4
+            if u < LATE or turn < 2:
                 vps = psV.tile([P, 512], F32, name="vps")
-                top = m // 4
-                for g in range(top + 1):
-                    nc.tensor.matmul_mx(
-                        out=vps[:],
-                        lhsT=wc[1][:, g, P * m : P * m + P].bitcast(FP8X4),
-                        lhsT_scale=wpl[:, 2 + g, P * m : P * m + P],
-                        rhs=uc[:, g, :].bitcast(FP8X4),
-                        rhs_scale=up[:, g, :],
-                        start=(g == 0),
-                        stop=(g == top),
-                    )
-                v_tiles[(q, m)] = vps
-
-        def resid(k):
-            q, mp = divmod(k, 4)
-            for m in (2 * mp, 2 * mp + 1):
-                ot = opool.tile([P, 4, D], F32, name="ot")
-                nc.vector.tensor_tensor(
-                    out=ot[:],
-                    in0=v_tiles[(q, m)][:].rearrange("p (b d) -> p b d", b=4),
-                    in1=xn[q][:, :, m, :],
-                    op=ALU.add,
+            elif turn == 2:
+                vps = psL.tile([P, 512], F32, name="lnw_ps")
+            else:
+                vps = psL.tile([P, 512], F32, name="lnb_ps")
+            top = m // 4
+            for g in range(top + 1):
+                nc.tensor.matmul_mx(
+                    out=vps[:],
+                    lhsT=wc[1][:, g, P * m : P * m + P].bitcast(FP8X4),
+                    lhsT_scale=wpl[:, 2 + g, P * m : P * m + P],
+                    rhs=uc[:, g, :].bitcast(FP8X4),
+                    rhs_scale=up[:, g, :],
+                    start=(g == 0),
+                    stop=(g == top),
                 )
-                nc.sync.dma_start(
-                    out=out[4 * q : 4 * q + 4, P * m : P * m + P, :].rearrange("b c d -> c b d"),
-                    in_=ot[:],
-                )
+            v_tiles[u] = vps
 
-        for b in range(4):
-            square(b)
-            if b == 1:
-                chain(0)
-            if b == 3:
-                chain(1)
-        for s in range(-2, 22):
-            if s >= 1 and (s + 3) % 4 == 0 and (s + 3) // 4 <= 3:
-                chain((s + 3) // 4 + 1)
-            for b in range(4, B):
-                if max(-2, b - 7) == s:
-                    square(b)
-            if s + 2 < B:
-                ln(s + 2)
-            if 0 <= s + 1 < B:
-                quant_h(s + 1)
-                mm1(s + 1)
+        def resid(u):
+            q, m = divmod(u, 8)
+            ot = opool.tile([P, 4, D], F32, name="ot")
+            nc.vector.tensor_tensor(
+                out=ot[:],
+                in0=v_tiles[u][:].rearrange("p (b d) -> p b d", b=4),
+                in1=xn[q][:, :, m, :],
+                op=ALU.add,
+            )
+            nc.sync.dma_start(
+                out=out[4 * q : 4 * q + 4, P * m : P * m + P, :].rearrange("b c d -> c b d"),
+                in_=ot[:],
+            )
+
+        state = {"mm2": 0, "res": 0, "qu": 0}
+
+        def feed_mm2():
+            while state["mm2"] < 32:
+                u = state["mm2"]
+                need = 2 * (u // 8) + (1 if u % 8 < 4 else 2)
+                room = 2 if u < LATE else 4
+                if u - state["res"] >= room or state["qu"] < need:
+                    break
+                mm2(u)
+                state["mm2"] = u + 1
+
+        def do_resid(n):
+            for i in range(n):
+                resid(state["res"])
+                state["res"] = state["res"] + 1
+                feed_mm2()
+
+        def do_quant_u(q, g):
+            quant_u(q, g)
+            state["qu"] = 2 * q + g + 1
+            feed_mm2()
+
+        square(0)
+        chain_a(0)
+        square(1)
+        chain_a(1)
+        place_ln()
+        chain_s(0)
+        chain_c(0)
+        chain_s(1)
+        square(2)
+        square(3)
+        chain_a(2)
+        for s in range(-3, 18):
             if 0 <= s < B:
                 hs2(s)
-            if s >= 5 and (s - 5) % 4 == 0 and (s - 5) // 4 <= 3:
-                quant_u((s - 5) // 4)
-            if 0 <= s - 6 < 16:
-                resid(s - 6)
-            if 0 <= s - 5 < 16:
-                mm2(s - 5)
+            if 0 <= s + 1 < B:
+                mm1(s + 1)
+            if 0 <= s < B:
+                transp(s)
+            first, second = RES_AT.get(s, (0, 0))
+            do_resid(first)
+            for k in range(len(GROUPS)):
+                if CS.get(k) == s:
+                    chain_s(k)
+            if s + 3 < B and (s + 3) not in GB:
+                ln(s + 3)
+            do_resid(second)
+            if 0 <= s + 2 < B:
+                quant_h(s + 2)
+            for k in range(len(GROUPS)):
+                if CC.get(k) == s:
+                    chain_c(k)
+            if s >= 4 and (s - 4) % 4 == 0 and (s - 4) // 4 <= 3:
+                do_quant_u((s - 4) // 4, 0)
+                do_quant_u((s - 4) // 4, 1)
+            for b in SQ.get(s, ()):
+                square(b)
+            for k in range(len(GROUPS)):
+                if CA.get(k) == s:
+                    chain_a(k)
+            for b in GR.get(s, ()):
+                g_route(b)

@@ -255,21 +255,19 @@ def tile_timemixing_kernel(tc, x, ln_w, ln_b, W1_words, W1_scales, W2_words, W2_
                         start=(g == 0),
                         stop=(g == tcn),
                     )
-                r = rpool.tile([P, 4, P], F32, name="r")
-                nc.scalar.activation(
-                    out=r[:], in_=acc[:].rearrange("p (q j) -> p j q", j=4), func=ACT.Relu, bias=0.5, scale=1.0 / 6.0
-                )
+                r = rpool.tile([P, 512], F32, name="r")
+                nc.scalar.activation(out=r[:], in_=acc[:], func=ACT.Relu, bias=0.5, scale=1.0 / 6.0)
                 acc_tiles[(b, tcn)] = acc
                 r_tiles[(b, tcn)] = r
 
         def hs2(b):
-            uT = work.tile([P, 2, 4, P], BF16, name="uT")
+            uT = work.tile([P, 2, 512], BF16, name="uT")
             for tcn in range(2):
                 nc.vector.scalar_tensor_tensor(
                     out=uT[:, tcn],
                     in0=r_tiles[(b, tcn)][:],
                     scalar=1.0,
-                    in1=acc_tiles[(b, tcn)][:].rearrange("p (q j) -> p j q", j=4),
+                    in1=acc_tiles[(b, tcn)][:],
                     op0=ALU.min,
                     op1=ALU.mult,
                 )
@@ -285,7 +283,7 @@ def tile_timemixing_kernel(tc, x, ln_w, ln_b, W1_words, W1_scales, W2_words, W2_
             tp = psT.tile([P, 2, 4, D], BF16, name="tp")
             for g in range(2):
                 for j in range(4):
-                    nc.tensor.transpose(out=tp[:, g, j, :], in_=uT[:, g, j, :], identity=ident[:])
+                    nc.tensor.transpose(out=tp[:, g, j, :], in_=uT[:, g, j:512:4], identity=ident[:])
             for g in range(2):
                 nc.scalar.copy(out=ug[:, g, bl, :, :], in_=tp[:, g].rearrange("p j d -> p d j"))
 

@@ -19,15 +19,7 @@ NTOT = S * D
 FLOPS = 2 * 2 * S * S * B * D
 
 MANUAL = False
-GB = [3,6,8,10,12,13,14]
-GROUPS = [[0], [1], [2, 3], [4, 5, 6, 7], [8, 9, 10, 11], [12, 13, 14, 15]]
-RES_AT = {5: (1, 1), 6: (1, 1), 7: (1, 1), 8: (1, 1), 9: (1, 1), 10: (1, 1), 11: (1, 1), 12: (1, 1), 13: (2, 0), 14: (2, 0), 15: (2, 0), 16: (2, 0), 17: (8, 0)}
-SQ = {-3: (4, 5, 6), -2: (7,), -1: (8, 9), 0: (10, 11), 1: (12, 13), 2: (14, 15)}
-CA = {3: -2, 4: 0, 5: 2}
-CS = {2: -3, 3: -1, 4: 1, 5: 3}
-CC = {1: -3, 2: -2, 3: -1, 4: 1, 5: 3}
-GR = {-2: (3,), -1: (6,), 1: (8, 10), 3: (12, 13, 14)}
-LATE = 16
+GROUPS = [[0, 1], [2, 3], [4, 5, 6, 7], [8, 9, 10, 11], [12, 13, 14, 15]]
 
 
 def tile_timemixing_kernel(tc, x, ln_w, ln_b, W1_words, W1_scales, W2_words, W2_scales, out):
@@ -35,16 +27,15 @@ def tile_timemixing_kernel(tc, x, ln_w, ln_b, W1_words, W1_scales, W2_words, W2_
     with ExitStack() as ctx:
         ctx.enter_context(nc.allow_non_contiguous_dma(reason="rows of 256 B to 2 KiB"))
         keep = ctx.enter_context(tc.tile_pool(name="keep", bufs=1))
-        small = ctx.enter_context(tc.tile_pool(name="small", bufs=3))
+        small = ctx.enter_context(tc.tile_pool(name="small", bufs=2))
         work = ctx.enter_context(tc.tile_pool(name="work", bufs=3))
-        gpool = ctx.enter_context(tc.tile_pool(name="gpool", bufs=2))
         rpool = ctx.enter_context(tc.tile_pool(name="rpool", bufs=4))
         upool = ctx.enter_context(tc.tile_pool(name="upool", bufs=2))
-        opool = ctx.enter_context(tc.tile_pool(name="opool", bufs=8))
-        psL = ctx.enter_context(tc.psum_pool(name="psL", bufs=1))
-        psA = ctx.enter_context(tc.psum_pool(name="psA", bufs=3))
+        opool = ctx.enter_context(tc.tile_pool(name="opool", bufs=4))
+        psA = ctx.enter_context(tc.psum_pool(name="psA", bufs=4))
         psT = ctx.enter_context(tc.psum_pool(name="psT", bufs=1))
         psV = ctx.enter_context(tc.psum_pool(name="psV", bufs=2))
+        psS = ctx.enter_context(tc.psum_pool(name="psS", bufs=1))
         if MANUAL:
             ctx.enter_context(tc.manual_schedule())
 
@@ -59,8 +50,8 @@ def tile_timemixing_kernel(tc, x, ln_w, ln_b, W1_words, W1_scales, W2_words, W2_
         warm = keep.tile([P, 1], F32, name="warm")
         nc.scalar.activation(out=warm[:], in_=ones_f[:, 0:1], func=ACT.Sqrt)
 
-        stat = [keep.tile([P, 2 * len(GROUPS[k])], F32, name="stat%d" % k) for k in range(len(GROUPS))]
-        negmean_all = keep.tile([P, B], F32, name="negmean_all")
+        sq_all = keep.tile([P, B], F32, name="sq_all")
+        mean_all = keep.tile([P, B], F32, name="mean_all")
         rstd_all = keep.tile([P, B], F32, name="rstd_all")
 
         xq = [keep.tile([P, S], BF16, name="xq%d" % b) for b in range(B)]
@@ -97,44 +88,34 @@ def tile_timemixing_kernel(tc, x, ln_w, ln_b, W1_words, W1_scales, W2_words, W2_
                 in_=words[1].rearrange("p n t -> p (n t)").bitcast(I32)[:, 512:S],
             )
 
-        load_xq(0)
-        load_xq(1)
+        for b in range(4):
+            load_xq(b)
         for dst, src in ((lnw, ln_w), (lnb, ln_b)):
             nc.sync.dma_start(
                 out=dst[:].rearrange("p (g c) -> p g c", g=2),
                 in_=src.rearrange("(g p j) d -> p g (j d)", g=2, p=P, j=4),
             )
-        load_xq(2)
-        load_xq(3)
         load_w(0, W1_words, W1_scales)
-        for b in range(4, B):
+        for b in range(4, 8):
             load_xq(b)
         load_w(1, W2_words, W2_scales)
-        for q in range(4):
+        for b in range(8, 12):
+            load_xq(b)
+        load_xn(0)
+        for b in range(12, 16):
+            load_xq(b)
+        for q in range(1, 4):
             load_xn(q)
 
         lnw_g = keep.tile([P, 2, D, 4], BF16, name="lnw_g")
         lnb_g = keep.tile([P, 2, D, 4], BF16, name="lnb_g")
-        lnw_ps = psL.tile([P, 2, D, 4], BF16, name="lnw_ps")
-        lnb_ps = psL.tile([P, 2, D, 4], BF16, name="lnb_ps")
-
-        def place_ln():
-            for nat, grouped, bank in ((lnw, lnw_g, lnw_ps), (lnb, lnb_g, lnb_ps)):
-                nc.vector.tensor_copy(out=grouped[:], in_=nat[:].rearrange("p (g j d) -> p g d j", g=2, j=4))
-                for g in range(2):
-                    nc.tensor.matmul(
-                        out=bank[:, g].rearrange("p d j -> p (d j)"),
-                        lhsT=ident[:],
-                        rhs=grouped[:, g].rearrange("p d j -> p (d j)"),
-                        start=True,
-                        stop=True,
-                    )
+        nc.vector.tensor_copy(out=lnw_g[:], in_=lnw[:].rearrange("p (g j d) -> p g d j", g=2, j=4))
+        nc.vector.tensor_copy(out=lnb_g[:], in_=lnb[:].rearrange("p (g j d) -> p g d j", g=2, j=4))
 
         hc = [keep.tile([P, 2 * D], U32, align_bytes=64, name="hc%d" % b) for b in range(B)]
         hp = [keep.tile([P, 2 * D], U8, align_bytes=64, name="hp%d" % b) for b in range(B)]
 
         st_tiles = {}
-        ch_tiles = {}
         hg_tiles = {}
         acc_tiles = {}
         r_tiles = {}
@@ -148,12 +129,12 @@ def tile_timemixing_kernel(tc, x, ln_w, ln_b, W1_words, W1_scales, W2_words, W2_
             k = group_of(b)
             grp = GROUPS[k]
             if b == grp[0]:
-                st_new = psV.tile([P, 512], F32, name="vps")
-                st_tiles[k] = st_new
+                st = psS.tile([P, 32], F32, name="st")
+                st_tiles[k] = st
             st = st_tiles[k]
-            bl = b - grp[0]
             junk = work.tile([P, S], BF16, name="junk")
-            nc.scalar.activation(out=junk[:], in_=xq[b][:], func=ACT.Square, accum_out=stat[k][:, bl : bl + 1])
+            nc.scalar.activation(out=junk[:], in_=xq[b][:], func=ACT.Square, accum_out=sq_all[:, b : b + 1])
+            bl = b - grp[0]
             for c in range(8):
                 nc.tensor.matmul(
                     out=st[:, 2 * bl : 2 * bl + 2],
@@ -163,39 +144,27 @@ def tile_timemixing_kernel(tc, x, ln_w, ln_b, W1_words, W1_scales, W2_words, W2_
                     stop=(c == 7),
                 )
 
-        def chain_a(k):
-            n = len(GROUPS[k])
-            st = st_tiles[k]
-            nc.scalar.copy(out=stat[k][:, n : 2 * n], in_=st[:, 0 : 2 * n : 2])
-            nc.tensor.matmul(out=st[:, 16 : 16 + 2 * n], lhsT=ones_f[:], rhs=stat[k][:], start=True, stop=True)
-
-        def chain_s(k):
+        def chain(k):
             grp = GROUPS[k]
             n = len(grp)
             b0 = grp[0]
             st = st_tiles[k]
-            sums = st[:, 16 + n : 16 + 2 * n]
-            nc.scalar.activation(out=negmean_all[:, b0 : b0 + n], in_=sums, func=ACT.Copy, scale=-1.0 / NTOT)
+            cs_sb = small.tile([P, 4], F32, name="cs_sb")
+            nc.vector.tensor_copy(out=cs_sb[:, 0:n], in_=st[:, 0 : 2 * n : 2])
+            nc.tensor.matmul(out=st[:, 16 : 16 + n], lhsT=ones_f[:], rhs=cs_sb[:, 0:n], start=True, stop=True)
+            nc.tensor.matmul(out=st[:, 24 : 24 + n], lhsT=ones_f[:], rhs=sq_all[:, b0 : b0 + n], start=True, stop=True)
+            mean = mean_all[:, b0 : b0 + n]
+            nc.vector.tensor_scalar(out=mean, in0=st[:, 16 : 16 + n], scalar1=1.0 / NTOT, scalar2=None, op0=ALU.mult)
+            ve = small.tile([P, 4], F32, name="ve")
+            nc.vector.tensor_scalar(
+                out=ve[:, 0:n], in0=st[:, 24 : 24 + n], scalar1=1.0 / NTOT, scalar2=EPS, op0=ALU.mult, op1=ALU.add
+            )
             msq = small.tile([P, 4], F32, name="msq")
-            nc.scalar.activation(out=msq[:, 0:n], in_=sums, func=ACT.Square, scale=1.0 / NTOT)
-            shift = small.tile([P, 4], F32, name="shift")
-            nc.scalar.activation(out=shift[:, 0:n], in_=msq[:, 0:n], func=ACT.Identity, scale=-1.0, bias=EPS)
+            nc.vector.tensor_tensor(out=msq[:, 0:n], in0=mean, in1=mean, op=ALU.mult)
+            nc.vector.tensor_tensor(out=ve[:, 0:n], in0=ve[:, 0:n], in1=msq[:, 0:n], op=ALU.subtract)
             std = small.tile([P, 4], F32, name="std")
-            for i in range(n):
-                nc.scalar.activation(
-                    out=std[:, i : i + 1],
-                    in_=st[:, 16 + i : 17 + i],
-                    func=ACT.Sqrt,
-                    scale=1.0 / NTOT,
-                    bias=shift[:, i : i + 1],
-                )
-            ch_tiles[k] = std
-
-        def chain_c(k):
-            grp = GROUPS[k]
-            n = len(grp)
-            b0 = grp[0]
-            nc.vector.reciprocal(out=rstd_all[:, b0 : b0 + n], in_=ch_tiles[k][:, 0:n])
+            nc.scalar.activation(out=std[:, 0:n], in_=ve[:, 0:n], func=ACT.Sqrt)
+            nc.vector.reciprocal(out=rstd_all[:, b0 : b0 + n], in_=std[:, 0:n])
 
         def ln(b):
             t = work.tile([P, 2, D, 4], F32, name="t")
@@ -203,9 +172,9 @@ def tile_timemixing_kernel(tc, x, ln_w, ln_b, W1_words, W1_scales, W2_words, W2_
                 nc.vector.scalar_tensor_tensor(
                     out=t[:, g],
                     in0=xq[b][:, 512 * g : 512 * g + 512].rearrange("p (j d) -> p d j", j=4),
-                    scalar=negmean_all[:, b : b + 1],
-                    in1=lnw_ps[:, g],
-                    op0=ALU.add,
+                    scalar=mean_all[:, b : b + 1],
+                    in1=lnw_g[:, g],
+                    op0=ALU.subtract,
                     op1=ALU.mult,
                 )
             hg = work.tile([P, 2, D, 4], BF16, align_bytes=64, name="hg")
@@ -213,27 +182,11 @@ def tile_timemixing_kernel(tc, x, ln_w, ln_b, W1_words, W1_scales, W2_words, W2_
                 out=hg[:].rearrange("p g d j -> p (g d j)"),
                 in0=t[:].rearrange("p g d j -> p (g d j)"),
                 scalar=rstd_all[:, b : b + 1],
-                in1=lnb_ps[:].rearrange("p g d j -> p (g d j)"),
+                in1=lnb_g[:].rearrange("p g d j -> p (g d j)"),
                 op0=ALU.mult,
                 op1=ALU.add,
             )
             hg_tiles[b] = hg
-
-        def g_route(b):
-            xg = gpool.tile([P, 2, D, 4], F32, name="xg")
-            hgg = keep.tile([P, 2, D, 4], BF16, align_bytes=64, name="hgg%d" % b)
-            for g in range(2):
-                nc.gpsimd.tensor_scalar(
-                    out=xg[:, g],
-                    in0=xq[b][:, 512 * g : 512 * g + 512].rearrange("p (j d) -> p d j", j=4),
-                    scalar1=negmean_all[:, b : b + 1],
-                    scalar2=rstd_all[:, b : b + 1],
-                    op0=ALU.add,
-                    op1=ALU.mult,
-                )
-                nc.gpsimd.tensor_tensor(out=xg[:, g], in0=xg[:, g], in1=lnw_g[:, g], op=ALU.mult)
-                nc.gpsimd.tensor_tensor(out=hgg[:, g], in0=xg[:, g], in1=lnb_g[:, g], op=ALU.add)
-            hg_tiles[b] = hgg
 
         def quant_h(b):
             nc.vector.quantize_mx(
@@ -255,148 +208,105 @@ def tile_timemixing_kernel(tc, x, ln_w, ln_b, W1_words, W1_scales, W2_words, W2_
                         start=(g == 0),
                         stop=(g == tcn),
                     )
-                r = rpool.tile([P, 512], F32, name="r")
-                nc.scalar.activation(out=r[:], in_=acc[:], func=ACT.Relu, bias=0.5, scale=1.0 / 6.0)
+                r = rpool.tile([P, 4, P], F32, name="r")
+                nc.scalar.activation(
+                    out=r[:], in_=acc[:].rearrange("p (q j) -> p j q", j=4), func=ACT.Relu, bias=0.5, scale=1.0 / 6.0
+                )
                 acc_tiles[(b, tcn)] = acc
                 r_tiles[(b, tcn)] = r
 
         def hs2(b):
-            uT = work.tile([P, 2, 512], BF16, name="uT")
+            uT = work.tile([P, 2, 4, P], BF16, name="uT")
             for tcn in range(2):
                 nc.vector.scalar_tensor_tensor(
                     out=uT[:, tcn],
                     in0=r_tiles[(b, tcn)][:],
                     scalar=1.0,
-                    in1=acc_tiles[(b, tcn)][:],
+                    in1=acc_tiles[(b, tcn)][:].rearrange("p (q j) -> p j q", j=4),
                     op0=ALU.min,
                     op1=ALU.mult,
                 )
-            u_tiles[("T", b)] = uT
-
-        def transp(b):
-            uT = u_tiles[("T", b)]
             q, bl = divmod(b, 4)
             if bl == 0:
-                ug_new = upool.tile([P, 2, 4, D, 4], BF16, align_bytes=64, name="ug")
-                u_tiles[q] = ug_new
+                ug = upool.tile([P, 2, 4, D, 4], BF16, align_bytes=64, name="ug")
+                u_tiles[q] = ug
             ug = u_tiles[q]
             tp = psT.tile([P, 2, 4, D], BF16, name="tp")
             for g in range(2):
                 for j in range(4):
-                    nc.tensor.transpose(out=tp[:, g, j, :], in_=uT[:, g, j:512:4], identity=ident[:])
+                    nc.tensor.transpose(
+                        out=tp[:, g, j, :],
+                        in_=uT[:, g, j, :],
+                        identity=ident[:],
+                    )
+            nc.scalar.copy(out=ug[:, :, bl, :, :], in_=tp[:].rearrange("p g j d -> p g d j"))
+
+        def quant_u(q):
+            uc = upool.tile([P, 2, 512], U32, align_bytes=64, name="uc")
+            up = upool.tile([P, 2, 512], U8, align_bytes=64, name="up")
             for g in range(2):
-                nc.scalar.copy(out=ug[:, g, bl, :, :], in_=tp[:, g].rearrange("p j d -> p d j"))
-
-        def quant_u(q, g):
-            if g == 0:
-                uc_new = upool.tile([P, 2, 512], U32, align_bytes=64, name="uc")
-                up_new = upool.tile([P, 2, 512], U8, align_bytes=64, name="up")
-                u_tiles[(q, "c")] = (uc_new, up_new)
-            uc, up = u_tiles[(q, "c")]
-            nc.vector.quantize_mx(
-                out=uc[:, g, :].bitcast(FP8X4),
-                scales=up[:, g, :],
-                in_=u_tiles[q][:, g].rearrange("p b d j -> p (b d j)"),
-            )
-
-        def mm2(u):
-            q, m = divmod(u, 8)
-            uc, up = u_tiles[(q, "c")]
-            turn = (u - LATE) % 4
-            if u < LATE or turn < 2:
-                vps = psV.tile([P, 512], F32, name="vps")
-            elif turn == 2:
-                vps = psL.tile([P, 512], F32, name="lnw_ps")
-            else:
-                vps = psL.tile([P, 512], F32, name="lnb_ps")
-            top = m // 4
-            for g in range(top + 1):
-                nc.tensor.matmul_mx(
-                    out=vps[:],
-                    lhsT=wc[1][:, g, P * m : P * m + P].bitcast(FP8X4),
-                    lhsT_scale=wpl[:, 2 + g, P * m : P * m + P],
-                    rhs=uc[:, g, :].bitcast(FP8X4),
-                    rhs_scale=up[:, g, :],
-                    start=(g == 0),
-                    stop=(g == top),
+                nc.vector.quantize_mx(
+                    out=uc[:, g, :].bitcast(FP8X4),
+                    scales=up[:, g, :],
+                    in_=u_tiles[q][:, g].rearrange("p b d j -> p (b d j)"),
                 )
-            v_tiles[u] = vps
+            u_tiles[(q, "c")] = (uc, up)
 
-        def resid(u):
-            q, m = divmod(u, 8)
-            ot = opool.tile([P, 4, D], F32, name="ot")
-            nc.vector.tensor_tensor(
-                out=ot[:],
-                in0=v_tiles[u][:].rearrange("p (b d) -> p b d", b=4),
-                in1=xn[q][:, :, m, :],
-                op=ALU.add,
-            )
-            nc.sync.dma_start(
-                out=out[4 * q : 4 * q + 4, P * m : P * m + P, :].rearrange("b c d -> c b d"),
-                in_=ot[:],
-            )
+        def mm2(k):
+            q, mp = divmod(k, 4)
+            uc, up = u_tiles[(q, "c")]
+            for m in (2 * mp, 2 * mp + 1):
+                vps = psV.tile([P, 512], F32, name="vps")
+                top = m // 4
+                for g in range(top + 1):
+                    nc.tensor.matmul_mx(
+                        out=vps[:],
+                        lhsT=wc[1][:, g, P * m : P * m + P].bitcast(FP8X4),
+                        lhsT_scale=wpl[:, 2 + g, P * m : P * m + P],
+                        rhs=uc[:, g, :].bitcast(FP8X4),
+                        rhs_scale=up[:, g, :],
+                        start=(g == 0),
+                        stop=(g == top),
+                    )
+                v_tiles[(q, m)] = vps
 
-        state = {"mm2": 0, "res": 0, "qu": 0}
+        def resid(k):
+            q, mp = divmod(k, 4)
+            for m in (2 * mp, 2 * mp + 1):
+                ot = opool.tile([P, 4, D], F32, name="ot")
+                nc.vector.tensor_tensor(
+                    out=ot[:],
+                    in0=v_tiles[(q, m)][:].rearrange("p (b d) -> p b d", b=4),
+                    in1=xn[q][:, :, m, :],
+                    op=ALU.add,
+                )
+                nc.sync.dma_start(
+                    out=out[4 * q : 4 * q + 4, P * m : P * m + P, :].rearrange("b c d -> c b d"),
+                    in_=ot[:],
+                )
 
-        def feed_mm2():
-            while state["mm2"] < 32:
-                u = state["mm2"]
-                need = 2 * (u // 8) + (1 if u % 8 < 4 else 2)
-                room = 2 if u < LATE else 4
-                if u - state["res"] >= room or state["qu"] < need:
-                    break
-                mm2(u)
-                state["mm2"] = u + 1
-
-        def do_resid(n):
-            for i in range(n):
-                resid(state["res"])
-                state["res"] = state["res"] + 1
-                feed_mm2()
-
-        def do_quant_u(q, g):
-            quant_u(q, g)
-            state["qu"] = 2 * q + g + 1
-            feed_mm2()
-
-        square(0)
-        chain_a(0)
-        square(1)
-        chain_a(1)
-        place_ln()
-        chain_s(0)
-        chain_c(0)
-        chain_s(1)
-        square(2)
-        square(3)
-        chain_a(2)
-        for s in range(-3, 18):
-            if 0 <= s < B:
-                hs2(s)
+        for b in range(4):
+            square(b)
+            if b == 1:
+                chain(0)
+            if b == 3:
+                chain(1)
+        for s in range(-2, 22):
+            if s >= 1 and (s + 3) % 4 == 0 and (s + 3) // 4 <= 3:
+                chain((s + 3) // 4 + 1)
+            for b in range(4, B):
+                if max(-2, b - 7) == s:
+                    square(b)
+            if s + 2 < B:
+                ln(s + 2)
             if 0 <= s + 1 < B:
+                quant_h(s + 1)
                 mm1(s + 1)
             if 0 <= s < B:
-                transp(s)
-            first, second = RES_AT.get(s, (0, 0))
-            do_resid(first)
-            for k in range(len(GROUPS)):
-                if CS.get(k) == s:
-                    chain_s(k)
-            if s + 3 < B and (s + 3) not in GB:
-                ln(s + 3)
-            do_resid(second)
-            if 0 <= s + 2 < B:
-                quant_h(s + 2)
-            for k in range(len(GROUPS)):
-                if CC.get(k) == s:
-                    chain_c(k)
-            if s >= 4 and (s - 4) % 4 == 0 and (s - 4) // 4 <= 3:
-                do_quant_u((s - 4) // 4, 0)
-                do_quant_u((s - 4) // 4, 1)
-            for b in SQ.get(s, ()):
-                square(b)
-            for k in range(len(GROUPS)):
-                if CA.get(k) == s:
-                    chain_a(k)
-            for b in GR.get(s, ()):
-                g_route(b)
+                hs2(s)
+            if s >= 5 and (s - 5) % 4 == 0 and (s - 5) // 4 <= 3:
+                quant_u((s - 5) // 4)
+            if 0 <= s - 6 < 16:
+                resid(s - 6)
+            if 0 <= s - 5 < 16:
+                mm2(s - 5)

@@ -19,7 +19,15 @@ NTOT = S * D
 FLOPS = 2 * 2 * S * S * B * D
 
 MANUAL = False
-GROUPS = [[0, 1], [2, 3], [4, 5, 6, 7], [8, 9, 10, 11], [12, 13, 14, 15]]
+GB = [3,6,8,10,12,13,14]
+GROUPS = [[0], [1], [2, 3], [4, 5, 6, 7], [8, 9, 10, 11], [12, 13, 14, 15]]
+RES_AT = {5: (1, 1), 6: (1, 1), 7: (1, 1), 8: (1, 1), 9: (1, 1), 10: (1, 1), 11: (1, 1), 12: (1, 1), 13: (2, 0), 14: (2, 0), 15: (2, 0), 16: (2, 0), 17: (8, 0)}
+SQ = {-3: (4, 5, 6), -2: (7,), -1: (8, 9), 0: (10, 11), 1: (12, 13), 2: (14, 15)}
+CA = {3: -2, 4: 0, 5: 2}
+CS = {2: -3, 3: -1, 4: 1, 5: 3}
+CC = {1: -3, 2: -2, 3: -1, 4: 1, 5: 3}
+GR = {-2: (3,), -1: (6,), 1: (8, 10), 3: (12, 13, 14)}
+LATE = 16
 
 
 def tile_timemixing_kernel(tc, x, ln_w, ln_b, W1_words, W1_scales, W2_words, W2_scales, out):
@@ -27,15 +35,16 @@ def tile_timemixing_kernel(tc, x, ln_w, ln_b, W1_words, W1_scales, W2_words, W2_
     with ExitStack() as ctx:
         ctx.enter_context(nc.allow_non_contiguous_dma(reason="rows of 256 B to 2 KiB"))
         keep = ctx.enter_context(tc.tile_pool(name="keep", bufs=1))
-        small = ctx.enter_context(tc.tile_pool(name="small", bufs=2))
+        small = ctx.enter_context(tc.tile_pool(name="small", bufs=3))
         work = ctx.enter_context(tc.tile_pool(name="work", bufs=3))
+        gpool = ctx.enter_context(tc.tile_pool(name="gpool", bufs=2))
         rpool = ctx.enter_context(tc.tile_pool(name="rpool", bufs=4))
         upool = ctx.enter_context(tc.tile_pool(name="upool", bufs=2))
-        opool = ctx.enter_context(tc.tile_pool(name="opool", bufs=4))
+        opool = ctx.enter_context(tc.tile_pool(name="opool", bufs=8))
+        psL = ctx.enter_context(tc.psum_pool(name="psL", bufs=1))
         psA = ctx.enter_context(tc.psum_pool(name="psA", bufs=4))
         psT = ctx.enter_context(tc.psum_pool(name="psT", bufs=1))
         psV = ctx.enter_context(tc.psum_pool(name="psV", bufs=2))
-        psS = ctx.enter_context(tc.psum_pool(name="psS", bufs=1))
         if MANUAL:
             ctx.enter_context(tc.manual_schedule())
 
@@ -50,8 +59,8 @@ def tile_timemixing_kernel(tc, x, ln_w, ln_b, W1_words, W1_scales, W2_words, W2_
         warm = keep.tile([P, 1], F32, name="warm")
         nc.scalar.activation(out=warm[:], in_=ones_f[:, 0:1], func=ACT.Sqrt)
 
-        sq_all = keep.tile([P, B], F32, name="sq_all")
-        mean_all = keep.tile([P, B], F32, name="mean_all")
+        stat = [keep.tile([P, 2 * len(GROUPS[k])], F32, name="stat%d" % k) for k in range(len(GROUPS))]
+        negmean_all = keep.tile([P, B], F32, name="negmean_all")
         rstd_all = keep.tile([P, B], F32, name="rstd_all")
 
         xq = [keep.tile([P, S], BF16, name="xq%d" % b) for b in range(B)]
@@ -88,34 +97,43 @@ def tile_timemixing_kernel(tc, x, ln_w, ln_b, W1_words, W1_scales, W2_words, W2_
                 in_=words[1].rearrange("p n t -> p (n t)").bitcast(I32)[:, 512:S],
             )
 
-        for b in range(4):
-            load_xq(b)
+        load_xq(0)
+        load_xq(1)
         for dst, src in ((lnw, ln_w), (lnb, ln_b)):
             nc.sync.dma_start(
                 out=dst[:].rearrange("p (g c) -> p g c", g=2),
                 in_=src.rearrange("(g p j) d -> p g (j d)", g=2, p=P, j=4),
             )
+        load_xq(2)
+        load_xq(3)
         load_w(0, W1_words, W1_scales)
-        for b in range(4, 8):
+        for b in range(4, B):
             load_xq(b)
         load_w(1, W2_words, W2_scales)
-        for b in range(8, 12):
-            load_xq(b)
-        load_xn(0)
-        for b in range(12, 16):
-            load_xq(b)
-        for q in range(1, 4):
+        for q in range(4):
             load_xn(q)
 
         lnw_g = keep.tile([P, 2, D, 4], BF16, name="lnw_g")
         lnb_g = keep.tile([P, 2, D, 4], BF16, name="lnb_g")
-        nc.vector.tensor_copy(out=lnw_g[:], in_=lnw[:].rearrange("p (g j d) -> p g d j", g=2, j=4))
-        nc.vector.tensor_copy(out=lnb_g[:], in_=lnb[:].rearrange("p (g j d) -> p g d j", g=2, j=4))
+        lnw_ps = psL.tile([P, 2, D, 4], BF16, name="lnw_ps")
+
+        def place_ln():
+            for nat, grouped in ((lnw, lnw_g), (lnb, lnb_g)):
+                nc.vector.tensor_copy(out=grouped[:], in_=nat[:].rearrange("p (g j d) -> p g d j", g=2, j=4))
+            for g in range(2):
+                nc.tensor.matmul(
+                    out=lnw_ps[:, g].rearrange("p d j -> p (d j)"),
+                    lhsT=ident[:],
+                    rhs=lnw_g[:, g].rearrange("p d j -> p (d j)"),
+                    start=True,
+                    stop=True,
+                )
 
         hc = [keep.tile([P, 2 * D], U32, align_bytes=64, name="hc%d" % b) for b in range(B)]
         hp = [keep.tile([P, 2 * D], U8, align_bytes=64, name="hp%d" % b) for b in range(B)]
 
         st_tiles = {}
+        ch_tiles = {}
         hg_tiles = {}
         acc_tiles = {}
         r_tiles = {}
@@ -129,12 +147,12 @@ def tile_timemixing_kernel(tc, x, ln_w, ln_b, W1_words, W1_scales, W2_words, W2_
             k = group_of(b)
             grp = GROUPS[k]
             if b == grp[0]:
-                st = psS.tile([P, 32], F32, name="st")
-                st_tiles[k] = st
+                st_new = psV.tile([P, 512], F32, name="vps")
+                st_tiles[k] = st_new
             st = st_tiles[k]
-            junk = work.tile([P, S], BF16, name="junk")
-            nc.scalar.activation(out=junk[:], in_=xq[b][:], func=ACT.Square, accum_out=sq_all[:, b : b + 1])
             bl = b - grp[0]
+            junk = work.tile([P, S], BF16, name="junk")
+            nc.scalar.activation(out=junk[:], in_=xq[b][:], func=ACT.Square, accum_out=stat[k][:, bl : bl + 1])
             for c in range(8):
                 nc.tensor.matmul(
                     out=st[:, 2 * bl : 2 * bl + 2],
@@ -144,27 +162,39 @@ def tile_timemixing_kernel(tc, x, ln_w, ln_b, W1_words, W1_scales, W2_words, W2_
                     stop=(c == 7),
                 )
 
-        def chain(k):
+        def chain_a(k):
+            n = len(GROUPS[k])
+            st = st_tiles[k]
+            nc.scalar.copy(out=stat[k][:, n : 2 * n], in_=st[:, 0 : 2 * n : 2])
+            nc.tensor.matmul(out=st[:, 16 : 16 + 2 * n], lhsT=ones_f[:], rhs=stat[k][:], start=True, stop=True)
+
+        def chain_s(k):
             grp = GROUPS[k]
             n = len(grp)
             b0 = grp[0]
             st = st_tiles[k]
-            cs_sb = small.tile([P, 4], F32, name="cs_sb")
-            nc.vector.tensor_copy(out=cs_sb[:, 0:n], in_=st[:, 0 : 2 * n : 2])
-            nc.tensor.matmul(out=st[:, 16 : 16 + n], lhsT=ones_f[:], rhs=cs_sb[:, 0:n], start=True, stop=True)
-            nc.tensor.matmul(out=st[:, 24 : 24 + n], lhsT=ones_f[:], rhs=sq_all[:, b0 : b0 + n], start=True, stop=True)
-            mean = mean_all[:, b0 : b0 + n]
-            nc.vector.tensor_scalar(out=mean, in0=st[:, 16 : 16 + n], scalar1=1.0 / NTOT, scalar2=None, op0=ALU.mult)
-            ve = small.tile([P, 4], F32, name="ve")
-            nc.vector.tensor_scalar(
-                out=ve[:, 0:n], in0=st[:, 24 : 24 + n], scalar1=1.0 / NTOT, scalar2=EPS, op0=ALU.mult, op1=ALU.add
-            )
+            sums = st[:, 16 + n : 16 + 2 * n]
+            nc.scalar.activation(out=negmean_all[:, b0 : b0 + n], in_=sums, func=ACT.Copy, scale=-1.0 / NTOT)
             msq = small.tile([P, 4], F32, name="msq")
-            nc.vector.tensor_tensor(out=msq[:, 0:n], in0=mean, in1=mean, op=ALU.mult)
-            nc.vector.tensor_tensor(out=ve[:, 0:n], in0=ve[:, 0:n], in1=msq[:, 0:n], op=ALU.subtract)
+            nc.scalar.activation(out=msq[:, 0:n], in_=sums, func=ACT.Square, scale=1.0 / NTOT)
+            shift = small.tile([P, 4], F32, name="shift")
+            nc.scalar.activation(out=shift[:, 0:n], in_=msq[:, 0:n], func=ACT.Identity, scale=-1.0, bias=EPS)
             std = small.tile([P, 4], F32, name="std")
-            nc.scalar.activation(out=std[:, 0:n], in_=ve[:, 0:n], func=ACT.Sqrt)
-            nc.vector.reciprocal(out=rstd_all[:, b0 : b0 + n], in_=std[:, 0:n])
+            for i in range(n):
+                nc.scalar.activation(
+                    out=std[:, i : i + 1],
+                    in_=st[:, 16 + i : 17 + i],
+                    func=ACT.Sqrt,
+                    scale=1.0 / NTOT,
+                    bias=shift[:, i : i + 1],
+                )
+            ch_tiles[k] = std
+
+        def chain_c(k):
+            grp = GROUPS[k]
+            n = len(grp)
+            b0 = grp[0]
+            nc.vector.reciprocal(out=rstd_all[:, b0 : b0 + n], in_=ch_tiles[k][:, 0:n])
 
         def ln(b):
             t = work.tile([P, 2, D, 4], F32, name="t")
@@ -172,9 +202,9 @@ def tile_timemixing_kernel(tc, x, ln_w, ln_b, W1_words, W1_scales, W2_words, W2_
                 nc.vector.scalar_tensor_tensor(
                     out=t[:, g],
                     in0=xq[b][:, 512 * g : 512 * g + 512].rearrange("p (j d) -> p d j", j=4),
-                    scalar=mean_all[:, b : b + 1],
-                    in1=lnw_g[:, g],
-                    op0=ALU.subtract,
+                    scalar=negmean_all[:, b : b + 1],
+                    in1=lnw_ps[:, g],
+                    op0=ALU.add,
                     op1=ALU.mult,
                 )
             hg = work.tile([P, 2, D, 4], BF16, align_bytes=64, name="hg")
@@ -187,6 +217,22 @@ def tile_timemixing_kernel(tc, x, ln_w, ln_b, W1_words, W1_scales, W2_words, W2_
                 op1=ALU.add,
             )
             hg_tiles[b] = hg
+
+        def g_route(b):
+            xg = gpool.tile([P, 2, D, 4], F32, name="xg")
+            hgg = keep.tile([P, 2, D, 4], BF16, align_bytes=64, name="hgg%d" % b)
+            for g in range(2):
+                nc.gpsimd.tensor_scalar(
+                    out=xg[:, g],
+                    in0=xq[b][:, 512 * g : 512 * g + 512].rearrange("p (j d) -> p d j", j=4),
+                    scalar1=negmean_all[:, b : b + 1],
+                    scalar2=rstd_all[:, b : b + 1],
+                    op0=ALU.add,
+                    op1=ALU.mult,
+                )
+                nc.gpsimd.tensor_tensor(out=xg[:, g], in0=xg[:, g], in1=lnw_g[:, g], op=ALU.mult)
+                nc.gpsimd.tensor_tensor(out=hgg[:, g], in0=xg[:, g], in1=lnb_g[:, g], op=ALU.add)
+            hg_tiles[b] = hgg
 
         def quant_h(b):
             nc.vector.quantize_mx(
@@ -226,87 +272,129 @@ def tile_timemixing_kernel(tc, x, ln_w, ln_b, W1_words, W1_scales, W2_words, W2_
                     op0=ALU.min,
                     op1=ALU.mult,
                 )
+            u_tiles[("T", b)] = uT
+
+        def transp(b):
+            uT = u_tiles[("T", b)]
             q, bl = divmod(b, 4)
             if bl == 0:
-                ug = upool.tile([P, 2, 4, D, 4], BF16, align_bytes=64, name="ug")
-                u_tiles[q] = ug
+                ug_new = upool.tile([P, 2, 4, D, 4], BF16, align_bytes=64, name="ug")
+                u_tiles[q] = ug_new
             ug = u_tiles[q]
             tp = psT.tile([P, 2, 4, D], BF16, name="tp")
             for g in range(2):
                 for j in range(4):
-                    nc.tensor.transpose(
-                        out=tp[:, g, j, :],
-                        in_=uT[:, g, j, :],
-                        identity=ident[:],
-                    )
-            nc.scalar.copy(out=ug[:, :, bl, :, :], in_=tp[:].rearrange("p g j d -> p g d j"))
-
-        def quant_u(q):
-            uc = upool.tile([P, 2, 512], U32, align_bytes=64, name="uc")
-            up = upool.tile([P, 2, 512], U8, align_bytes=64, name="up")
+                    nc.tensor.transpose(out=tp[:, g, j, :], in_=uT[:, g, j, :], identity=ident[:])
             for g in range(2):
-                nc.vector.quantize_mx(
-                    out=uc[:, g, :].bitcast(FP8X4),
-                    scales=up[:, g, :],
-                    in_=u_tiles[q][:, g].rearrange("p b d j -> p (b d j)"),
-                )
-            u_tiles[(q, "c")] = (uc, up)
+                nc.scalar.copy(out=ug[:, g, bl, :, :], in_=tp[:, g].rearrange("p j d -> p d j"))
 
-        def mm2(k):
-            q, mp = divmod(k, 4)
+        def quant_u(q, g):
+            if g == 0:
+                uc_new = upool.tile([P, 2, 512], U32, align_bytes=64, name="uc")
+                up_new = upool.tile([P, 2, 512], U8, align_bytes=64, name="up")
+                u_tiles[(q, "c")] = (uc_new, up_new)
             uc, up = u_tiles[(q, "c")]
-            for m in (2 * mp, 2 * mp + 1):
+            nc.vector.quantize_mx(
+                out=uc[:, g, :].bitcast(FP8X4),
+                scales=up[:, g, :],
+                in_=u_tiles[q][:, g].rearrange("p b d j -> p (b d j)"),
+            )
+
+        def mm2(u):
+            q, m = divmod(u, 8)
+            uc, up = u_tiles[(q, "c")]
+            if u < LATE or (u - LATE) % 3 < 2:
                 vps = psV.tile([P, 512], F32, name="vps")
-                top = m // 4
-                for g in range(top + 1):
-                    nc.tensor.matmul_mx(
-                        out=vps[:],
-                        lhsT=wc[1][:, g, P * m : P * m + P].bitcast(FP8X4),
-                        lhsT_scale=wpl[:, 2 + g, P * m : P * m + P],
-                        rhs=uc[:, g, :].bitcast(FP8X4),
-                        rhs_scale=up[:, g, :],
-                        start=(g == 0),
-                        stop=(g == top),
-                    )
-                v_tiles[(q, m)] = vps
-
-        def resid(k):
-            q, mp = divmod(k, 4)
-            for m in (2 * mp, 2 * mp + 1):
-                ot = opool.tile([P, 4, D], F32, name="ot")
-                nc.vector.tensor_tensor(
-                    out=ot[:],
-                    in0=v_tiles[(q, m)][:].rearrange("p (b d) -> p b d", b=4),
-                    in1=xn[q][:, :, m, :],
-                    op=ALU.add,
+            else:
+                vps = psL.tile([P, 512], F32, name="lnw_ps")
+            top = m // 4
+            for g in range(top + 1):
+                nc.tensor.matmul_mx(
+                    out=vps[:],
+                    lhsT=wc[1][:, g, P * m : P * m + P].bitcast(FP8X4),
+                    lhsT_scale=wpl[:, 2 + g, P * m : P * m + P],
+                    rhs=uc[:, g, :].bitcast(FP8X4),
+                    rhs_scale=up[:, g, :],
+                    start=(g == 0),
+                    stop=(g == top),
                 )
-                nc.sync.dma_start(
-                    out=out[4 * q : 4 * q + 4, P * m : P * m + P, :].rearrange("b c d -> c b d"),
-                    in_=ot[:],
-                )
+            v_tiles[u] = vps
 
-        for b in range(4):
-            square(b)
-            if b == 1:
-                chain(0)
-            if b == 3:
-                chain(1)
-        for s in range(-2, 22):
-            if s >= 1 and (s + 3) % 4 == 0 and (s + 3) // 4 <= 3:
-                chain((s + 3) // 4 + 1)
-            for b in range(4, B):
-                if max(-2, b - 7) == s:
-                    square(b)
-            if s + 2 < B:
-                ln(s + 2)
-            if 0 <= s + 1 < B:
-                quant_h(s + 1)
-                mm1(s + 1)
+        def resid(u):
+            q, m = divmod(u, 8)
+            ot = opool.tile([P, 4, D], F32, name="ot")
+            nc.vector.tensor_tensor(
+                out=ot[:],
+                in0=v_tiles[u][:].rearrange("p (b d) -> p b d", b=4),
+                in1=xn[q][:, :, m, :],
+                op=ALU.add,
+            )
+            nc.sync.dma_start(
+                out=out[4 * q : 4 * q + 4, P * m : P * m + P, :].rearrange("b c d -> c b d"),
+                in_=ot[:],
+            )
+
+        state = {"mm2": 0, "res": 0, "qu": 0}
+
+        def feed_mm2():
+            while state["mm2"] < 32:
+                u = state["mm2"]
+                need = 2 * (u // 8) + (1 if u % 8 < 4 else 2)
+                room = 2 if u < LATE else 3
+                if u - state["res"] >= room or state["qu"] < need:
+                    break
+                mm2(u)
+                state["mm2"] = u + 1
+
+        def do_resid(n):
+            for i in range(n):
+                resid(state["res"])
+                state["res"] = state["res"] + 1
+                feed_mm2()
+
+        def do_quant_u(q, g):
+            quant_u(q, g)
+            state["qu"] = 2 * q + g + 1
+            feed_mm2()
+
+        square(0)
+        chain_a(0)
+        square(1)
+        chain_a(1)
+        place_ln()
+        chain_s(0)
+        chain_c(0)
+        chain_s(1)
+        square(2)
+        square(3)
+        chain_a(2)
+        for s in range(-3, 18):
             if 0 <= s < B:
                 hs2(s)
-            if s >= 5 and (s - 5) % 4 == 0 and (s - 5) // 4 <= 3:
-                quant_u((s - 5) // 4)
-            if 0 <= s - 6 < 16:
-                resid(s - 6)
-            if 0 <= s - 5 < 16:
-                mm2(s - 5)
+            if 0 <= s + 1 < B:
+                mm1(s + 1)
+            if 0 <= s < B:
+                transp(s)
+            first, second = RES_AT.get(s, (0, 0))
+            do_resid(first)
+            for k in range(len(GROUPS)):
+                if CS.get(k) == s:
+                    chain_s(k)
+            if s + 3 < B and (s + 3) not in GB:
+                ln(s + 3)
+            do_resid(second)
+            if 0 <= s + 2 < B:
+                quant_h(s + 2)
+            for k in range(len(GROUPS)):
+                if CC.get(k) == s:
+                    chain_c(k)
+            if s >= 4 and (s - 4) % 4 == 0 and (s - 4) // 4 <= 3:
+                do_quant_u((s - 4) // 4, 0)
+                do_quant_u((s - 4) // 4, 1)
+            for b in SQ.get(s, ()):
+                square(b)
+            for k in range(len(GROUPS)):
+                if CA.get(k) == s:
+                    chain_a(k)
+            for b in GR.get(s, ()):
+                g_route(b)

@@ -19,14 +19,14 @@ NTOT = S * D
 FLOPS = 2 * 2 * S * S * B * D
 
 MANUAL = False
-GB = [3,6,8,10,12,13,14]
+GB = []
 GROUPS = [[0], [1], [2, 3], [4, 5, 6, 7], [8, 9, 10, 11], [12, 13, 14, 15]]
 RES_AT = {5: (1, 1), 6: (1, 1), 7: (1, 1), 8: (1, 1), 9: (1, 1), 10: (1, 1), 11: (1, 1), 12: (1, 1), 13: (2, 0), 14: (2, 0), 15: (2, 0), 16: (2, 0), 17: (8, 0)}
 SQ = {-3: (4, 5, 6), -2: (7,), -1: (8, 9), 0: (10, 11), 1: (12, 13), 2: (14, 15)}
 CA = {3: -2, 4: 0, 5: 2}
 CS = {2: -3, 3: -1, 4: 1, 5: 3}
 CC = {1: -3, 2: -2, 3: -1, 4: 1, 5: 3}
-GR = {-2: (3,), -1: (6,), 1: (8, 10), 3: (12, 13, 14)}
+GR = {}
 LATE = 16
 
 
@@ -41,10 +41,9 @@ def tile_timemixing_kernel(tc, x, ln_w, ln_b, W1_words, W1_scales, W2_words, W2_
         rpool = ctx.enter_context(tc.tile_pool(name="rpool", bufs=4))
         upool = ctx.enter_context(tc.tile_pool(name="upool", bufs=2))
         opool = ctx.enter_context(tc.tile_pool(name="opool", bufs=8))
-        psL = ctx.enter_context(tc.psum_pool(name="psL", bufs=1))
         psA = ctx.enter_context(tc.psum_pool(name="psA", bufs=4))
         psT = ctx.enter_context(tc.psum_pool(name="psT", bufs=1))
-        psV = ctx.enter_context(tc.psum_pool(name="psV", bufs=2))
+        psV = ctx.enter_context(tc.psum_pool(name="psV", bufs=3))
         if MANUAL:
             ctx.enter_context(tc.manual_schedule())
 
@@ -115,19 +114,11 @@ def tile_timemixing_kernel(tc, x, ln_w, ln_b, W1_words, W1_scales, W2_words, W2_
 
         lnw_g = keep.tile([P, 2, D, 4], BF16, name="lnw_g")
         lnb_g = keep.tile([P, 2, D, 4], BF16, name="lnb_g")
-        lnw_ps = psL.tile([P, 2, D, 4], BF16, name="lnw_ps")
 
         def place_ln():
             for nat, grouped in ((lnw, lnw_g), (lnb, lnb_g)):
                 nc.vector.tensor_copy(out=grouped[:], in_=nat[:].rearrange("p (g j d) -> p g d j", g=2, j=4))
-            for g in range(2):
-                nc.tensor.matmul(
-                    out=lnw_ps[:, g].rearrange("p d j -> p (d j)"),
-                    lhsT=ident[:],
-                    rhs=lnw_g[:, g].rearrange("p d j -> p (d j)"),
-                    start=True,
-                    stop=True,
-                )
+
 
         hc = [keep.tile([P, 2 * D], U32, align_bytes=64, name="hc%d" % b) for b in range(B)]
         hp = [keep.tile([P, 2 * D], U8, align_bytes=64, name="hp%d" % b) for b in range(B)]
@@ -203,7 +194,7 @@ def tile_timemixing_kernel(tc, x, ln_w, ln_b, W1_words, W1_scales, W2_words, W2_
                     out=t[:, g],
                     in0=xq[b][:, 512 * g : 512 * g + 512].rearrange("p (j d) -> p d j", j=4),
                     scalar=negmean_all[:, b : b + 1],
-                    in1=lnw_ps[:, g],
+                    in1=lnw_g[:, g],
                     op0=ALU.add,
                     op1=ALU.mult,
                 )
@@ -303,10 +294,7 @@ def tile_timemixing_kernel(tc, x, ln_w, ln_b, W1_words, W1_scales, W2_words, W2_
         def mm2(u):
             q, m = divmod(u, 8)
             uc, up = u_tiles[(q, "c")]
-            if u < LATE or (u - LATE) % 3 < 2:
-                vps = psV.tile([P, 512], F32, name="vps")
-            else:
-                vps = psL.tile([P, 512], F32, name="lnw_ps")
+            vps = psV.tile([P, 512], F32, name="vps")
             top = m // 4
             for g in range(top + 1):
                 nc.tensor.matmul_mx(
@@ -340,7 +328,7 @@ def tile_timemixing_kernel(tc, x, ln_w, ln_b, W1_words, W1_scales, W2_words, W2_
             while state["mm2"] < 32:
                 u = state["mm2"]
                 need = 2 * (u // 8) + (1 if u % 8 < 4 else 2)
-                room = 2 if u < LATE else 3
+                room = 3
                 if u - state["res"] >= room or state["qu"] < need:
                     break
                 mm2(u)

@@ -187,7 +187,7 @@ def tile_timemixing_kernel(tc, x, ln_w, ln_b, W1_words, W1_scales, W2_words, W2_
             b0 = grp[0]
             nc.vector.reciprocal(out=rstd_all[:, b0 : b0 + n], in_=ch_tiles[k][:, 0:n])
 
-        def ln(b):
+        def ln_a(b):
             t = work.tile([P, 2, D, 4], F32, name="t")
             for g in range(2):
                 nc.vector.scalar_tensor_tensor(
@@ -198,10 +198,13 @@ def tile_timemixing_kernel(tc, x, ln_w, ln_b, W1_words, W1_scales, W2_words, W2_
                     op0=ALU.add,
                     op1=ALU.mult,
                 )
+            hg_tiles[("t", b)] = t
+
+        def ln_b(b):
             hg = work.tile([P, 2, D, 4], BF16, align_bytes=64, name="hg")
             nc.vector.scalar_tensor_tensor(
                 out=hg[:].rearrange("p g d j -> p (g d j)"),
-                in0=t[:].rearrange("p g d j -> p (g d j)"),
+                in0=hg_tiles[("t", b)][:].rearrange("p g d j -> p (g d j)"),
                 scalar=rstd_all[:, b : b + 1],
                 in1=lnb_g[:].rearrange("p g d j -> p (g d j)"),
                 op0=ALU.mult,
@@ -356,7 +359,7 @@ def tile_timemixing_kernel(tc, x, ln_w, ln_b, W1_words, W1_scales, W2_words, W2_
         square(2)
         square(3)
         chain_a(2)
-        for s in range(-3, 18):
+        for s in range(-4, 18):
             if 0 <= s < B:
                 hs2(s)
             if 0 <= s + 1 < B:
@@ -368,8 +371,10 @@ def tile_timemixing_kernel(tc, x, ln_w, ln_b, W1_words, W1_scales, W2_words, W2_
             for k in range(len(GROUPS)):
                 if CS.get(k) == s:
                     chain_s(k)
-            if s + 3 < B and (s + 3) not in GB:
-                ln(s + 3)
+            if 0 <= s + 4 < B:
+                ln_a(s + 4)
+            if 0 <= s + 3 < B:
+                ln_b(s + 3)
             do_resid(second)
             if 0 <= s + 2 < B:
                 quant_h(s + 2)

from contextlib import ExitStack

import concourse.mybir as mybir
from concourse.masks import make_identity

F32 = mybir.dt.float32
BF16 = mybir.dt.bfloat16
U32 = mybir.dt.uint32
U8 = mybir.dt.uint8
I32 = mybir.dt.int32
FP8X4 = mybir.dt.float8_e4m3fn_x4
ALU = mybir.AluOpType
ACT = mybir.ActivationFunctionType

B, S, D = 16, 1024, 128
P = 128
EPS = 1e-5
NTOT = S * D
FLOPS = 2 * 2 * S * S * B * D

MANUAL = False
GB = []
GROUPS = [[0], [1], [2, 3], [4, 5, 6, 7], [8, 9, 10, 11], [12, 13, 14, 15]]
RES_AT = {5: (1, 1), 6: (1, 1), 7: (1, 1), 8: (1, 1), 9: (1, 1), 10: (1, 1), 11: (1, 1), 12: (1, 1), 13: (2, 0), 14: (2, 0), 15: (2, 0), 16: (2, 0), 17: (8, 0)}
SQ = {-3: (4, 5, 6), -2: (7,), -1: (8, 9), 0: (10, 11), 1: (12, 13), 2: (14, 15)}
CA = {3: -2, 4: 0, 5: 2}
CS = {2: -3, 3: -1, 4: 1, 5: 3}
CC = {1: -3, 2: -2, 3: -1, 4: 1, 5: 3}
GR = {}
LATE = 16


def tile_timemixing_kernel(tc, x, ln_w, ln_b, W1_words, W1_scales, W2_words, W2_scales, out):
    nc = tc.nc
    with ExitStack() as ctx:
        ctx.enter_context(nc.allow_non_contiguous_dma(reason="rows of 256 B to 2 KiB"))
        keep = ctx.enter_context(tc.tile_pool(name="keep", bufs=1))
        small = ctx.enter_context(tc.tile_pool(name="small", bufs=3))
        work = ctx.enter_context(tc.tile_pool(name="work", bufs=3))
        gpool = ctx.enter_context(tc.tile_pool(name="gpool", bufs=2))
        rpool = ctx.enter_context(tc.tile_pool(name="rpool", bufs=4))
        upool = ctx.enter_context(tc.tile_pool(name="upool", bufs=2))
        opool = ctx.enter_context(tc.tile_pool(name="opool", bufs=8))
        psA = ctx.enter_context(tc.psum_pool(name="psA", bufs=4))
        psT = ctx.enter_context(tc.psum_pool(name="psT", bufs=1))
        psV = ctx.enter_context(tc.psum_pool(name="psV", bufs=3))
        if MANUAL:
            ctx.enter_context(tc.manual_schedule())

        wpl = keep.tile([P, 4, S], U8, align_bytes=64, name="wpl")
        nc.vector.memset(wpl[:].bitcast(I32), 0)
        ones_f = keep.tile([P, P], F32, name="ones_f")
        nc.vector.memset(ones_f[:], 1.0)
        ones_b = keep.tile([P, 2], BF16, name="ones_b")
        nc.vector.memset(ones_b[:], 1.0)
        ident = keep.tile([P, P], BF16, name="ident")
        make_identity(nc, ident[:])
        warm = keep.tile([P, 1], F32, name="warm")
        nc.scalar.activation(out=warm[:], in_=ones_f[:, 0:1], func=ACT.Sqrt)

        stat = [keep.tile([P, 2 * len(GROUPS[k])], F32, name="stat%d" % k) for k in range(len(GROUPS))]
        negmean_all = keep.tile([P, B], F32, name="negmean_all")
        rstd_all = keep.tile([P, B], F32, name="rstd_all")

        xq = [keep.tile([P, S], BF16, name="xq%d" % b) for b in range(B)]
        xn = [keep.tile([P, 4, 8, D], BF16, name="xn%d" % q) for q in range(4)]
        lnw = keep.tile([P, S], BF16, name="lnw")
        lnb = keep.tile([P, S], BF16, name="lnb")
        wc = [keep.tile([P, 2, S], U32, align_bytes=64, name="wc%d" % w) for w in range(2)]

        def load_xq(b):
            nc.sync.dma_start(
                out=xq[b][:].rearrange("p (g c) -> p g c", g=2),
                in_=x[b].rearrange("(g p j) d -> p g (j d)", g=2, p=P, j=4),
            )

        def load_xn(q):
            nc.sync.dma_start(
                out=xn[q][:].rearrange("c b m d -> c (b m) d"),
                in_=x[4 * q : 4 * q + 4].rearrange("b (m c) d -> c (b m) d", c=P),
            )

        def load_w(w, words, scales):
            by_row = scales.rearrange("g (q r) n -> r q g n", r=4)
            for r in range(4):
                nc.sync.dma_start(
                    out=wpl[r:P:32, 2 * w : 2 * w + 2, :].bitcast(I32),
                    in_=by_row[r].bitcast(I32),
                )
            nc.sync.dma_start(
                out=wc[w][:, 0, :].bitcast(I32),
                in_=words[0].rearrange("p n t -> p (n t)").bitcast(I32),
            )
            nc.sync.dma_start(
                out=wc[w][:, 1, 512:S].bitcast(I32),
                in_=words[1].rearrange("p n t -> p (n t)").bitcast(I32)[:, 512:S],
            )

        load_xq(0)
        load_xq(1)
        for dst, src in ((lnw, ln_w), (lnb, ln_b)):
            nc.sync.dma_start(
                out=dst[:].rearrange("p (g c) -> p g c", g=2),
                in_=src.rearrange("(g p j) d -> p g (j d)", g=2, p=P, j=4),
            )
        load_xq(2)
        load_xq(3)
        load_w(0, W1_words, W1_scales)
        for b in range(4, B):
            load_xq(b)
        load_w(1, W2_words, W2_scales)
        for q in range(4):
            load_xn(q)

        lnw_g = keep.tile([P, 2, D, 4], BF16, name="lnw_g")
        lnb_g = keep.tile([P, 2, D, 4], BF16, name="lnb_g")

        def place_ln():
            for nat, grouped in ((lnw, lnw_g), (lnb, lnb_g)):
                nc.vector.tensor_copy(out=grouped[:], in_=nat[:].rearrange("p (g j d) -> p g d j", g=2, j=4))


        hc = [keep.tile([P, 2 * D], U32, align_bytes=64, name="hc%d" % b) for b in range(B)]
        hp = [keep.tile([P, 2 * D], U8, align_bytes=64, name="hp%d" % b) for b in range(B)]

        st_tiles = {}
        ch_tiles = {}
        hg_tiles = {}
        acc_tiles = {}
        r_tiles = {}
        u_tiles = {}
        v_tiles = {}

        def group_of(b):
            return [k for k in range(len(GROUPS)) if b in GROUPS[k]][0]

        def square(b):
            k = group_of(b)
            grp = GROUPS[k]
            if b == grp[0]:
                st_new = psV.tile([P, 512], F32, name="vps")
                st_tiles[k] = st_new
            st = st_tiles[k]
            bl = b - grp[0]
            junk = work.tile([P, S], BF16, name="junk")
            nc.scalar.activation(out=junk[:], in_=xq[b][:], func=ACT.Square, accum_out=stat[k][:, bl : bl + 1])
            for c in range(8):
                nc.tensor.matmul(
                    out=st[:, 2 * bl : 2 * bl + 2],
                    lhsT=xq[b][:, P * c : P * c + P],
                    rhs=ones_b[:],
                    start=(c == 0),
                    stop=(c == 7),
                )

        def chain_a(k):
            n = len(GROUPS[k])
            st = st_tiles[k]
            nc.scalar.copy(out=stat[k][:, n : 2 * n], in_=st[:, 0 : 2 * n : 2])
            nc.tensor.matmul(out=st[:, 16 : 16 + 2 * n], lhsT=ones_f[:], rhs=stat[k][:], start=True, stop=True)

        def chain_s(k):
            grp = GROUPS[k]
            n = len(grp)
            b0 = grp[0]
            st = st_tiles[k]
            sums = st[:, 16 + n : 16 + 2 * n]
            nc.scalar.activation(out=negmean_all[:, b0 : b0 + n], in_=sums, func=ACT.Copy, scale=-1.0 / NTOT)
            msq = small.tile([P, 4], F32, name="msq")
            nc.scalar.activation(out=msq[:, 0:n], in_=sums, func=ACT.Square, scale=1.0 / NTOT)
            shift = small.tile([P, 4], F32, name="shift")
            nc.scalar.activation(out=shift[:, 0:n], in_=msq[:, 0:n], func=ACT.Identity, scale=-1.0, bias=EPS)
            std = small.tile([P, 4], F32, name="std")
            for i in range(n):
                nc.scalar.activation(
                    out=std[:, i : i + 1],
                    in_=st[:, 16 + i : 17 + i],
                    func=ACT.Sqrt,
                    scale=1.0 / NTOT,
                    bias=shift[:, i : i + 1],
                )
            ch_tiles[k] = std

        def chain_c(k):
            grp = GROUPS[k]
            n = len(grp)
            b0 = grp[0]
            nc.vector.reciprocal(out=rstd_all[:, b0 : b0 + n], in_=ch_tiles[k][:, 0:n])

        def ln_a(b):
            t = work.tile([P, 2, D, 4], F32, name="t")
            for g in range(2):
                nc.vector.scalar_tensor_tensor(
                    out=t[:, g],
                    in0=xq[b][:, 512 * g : 512 * g + 512].rearrange("p (j d) -> p d j", j=4),
                    scalar=negmean_all[:, b : b + 1],
                    in1=lnw_g[:, g],
                    op0=ALU.add,
                    op1=ALU.mult,
                )
            hg_tiles[("t", b)] = t

        def ln_b(b):
            hg = work.tile([P, 2, D, 4], BF16, align_bytes=64, name="hg")
            nc.vector.scalar_tensor_tensor(
                out=hg[:].rearrange("p g d j -> p (g d j)"),
                in0=hg_tiles[("t", b)][:].rearrange("p g d j -> p (g d j)"),
                scalar=rstd_all[:, b : b + 1],
                in1=lnb_g[:].rearrange("p g d j -> p (g d j)"),
                op0=ALU.mult,
                op1=ALU.add,
            )
            hg_tiles[b] = hg

        def g_route(b):
            xg = gpool.tile([P, 2, D, 4], F32, name="xg")
            hgg = keep.tile([P, 2, D, 4], BF16, align_bytes=64, name="hgg%d" % b)
            for g in range(2):
                nc.gpsimd.tensor_scalar(
                    out=xg[:, g],
                    in0=xq[b][:, 512 * g : 512 * g + 512].rearrange("p (j d) -> p d j", j=4),
                    scalar1=negmean_all[:, b : b + 1],
                    scalar2=rstd_all[:, b : b + 1],
                    op0=ALU.add,
                    op1=ALU.mult,
                )
                nc.gpsimd.tensor_tensor(out=xg[:, g], in0=xg[:, g], in1=lnw_g[:, g], op=ALU.mult)
                nc.gpsimd.tensor_tensor(out=hgg[:, g], in0=xg[:, g], in1=lnb_g[:, g], op=ALU.add)
            hg_tiles[b] = hgg

        def quant_h(b):
            nc.vector.quantize_mx(
                out=hc[b][:].bitcast(FP8X4),
                scales=hp[b][:],
                in_=hg_tiles[b][:].rearrange("p g d j -> p (g d j)"),
            )

        def mm1(b):
            for tcn in range(2):
                acc = psA.tile([P, 512], F32, name="acc")
                for g in range(tcn + 1):
                    nc.tensor.matmul_mx(
                        out=acc[:],
                        lhsT=hc[b][:, D * g : D * g + D].bitcast(FP8X4),
                        lhsT_scale=hp[b][:, D * g : D * g + D],
                        rhs=wc[0][:, g, 512 * tcn : 512 * tcn + 512].bitcast(FP8X4),
                        rhs_scale=wpl[:, g, 512 * tcn : 512 * tcn + 512],
                        start=(g == 0),
                        stop=(g == tcn),
                    )
                r = rpool.tile([P, 4, P], F32, name="r")
                nc.scalar.activation(
                    out=r[:], in_=acc[:].rearrange("p (q j) -> p j q", j=4), func=ACT.Relu, bias=0.5, scale=1.0 / 6.0
                )
                acc_tiles[(b, tcn)] = acc
                r_tiles[(b, tcn)] = r

        def hs2(b):
            uT = work.tile([P, 2, 4, P], BF16, name="uT")
            for tcn in range(2):
                nc.vector.scalar_tensor_tensor(
                    out=uT[:, tcn],
                    in0=r_tiles[(b, tcn)][:],
                    scalar=1.0,
                    in1=acc_tiles[(b, tcn)][:].rearrange("p (q j) -> p j q", j=4),
                    op0=ALU.min,
                    op1=ALU.mult,
                )
            u_tiles[("T", b)] = uT

        def transp(b):
            uT = u_tiles[("T", b)]
            q, bl = divmod(b, 4)
            if bl == 0:
                ug_new = upool.tile([P, 2, 4, D, 4], BF16, align_bytes=64, name="ug")
                u_tiles[q] = ug_new
            ug = u_tiles[q]
            tp = psT.tile([P, 2, 4, D], BF16, name="tp")
            for g in range(2):
                for j in range(4):
                    nc.tensor.transpose(out=tp[:, g, j, :], in_=uT[:, g, j, :], identity=ident[:])
            for g in range(2):
                nc.scalar.copy(out=ug[:, g, bl, :, :], in_=tp[:, g].rearrange("p j d -> p d j"))

        def quant_u(q, g):
            if g == 0:
                uc_new = upool.tile([P, 2, 512], U32, align_bytes=64, name="uc")
                up_new = upool.tile([P, 2, 512], U8, align_bytes=64, name="up")
                u_tiles[(q, "c")] = (uc_new, up_new)
            uc, up = u_tiles[(q, "c")]
            nc.vector.quantize_mx(
                out=uc[:, g, :].bitcast(FP8X4),
                scales=up[:, g, :],
                in_=u_tiles[q][:, g].rearrange("p b d j -> p (b d j)"),
            )

        def mm2(u):
            q, m = divmod(u, 8)
            uc, up = u_tiles[(q, "c")]
            vps = psV.tile([P, 512], F32, name="vps")
            top = m // 4
            for g in range(top + 1):
                nc.tensor.matmul_mx(
                    out=vps[:],
                    lhsT=wc[1][:, g, P * m : P * m + P].bitcast(FP8X4),
                    lhsT_scale=wpl[:, 2 + g, P * m : P * m + P],
                    rhs=uc[:, g, :].bitcast(FP8X4),
                    rhs_scale=up[:, g, :],
                    start=(g == 0),
                    stop=(g == top),
                )
            v_tiles[u] = vps

        def resid(u):
            q, m = divmod(u, 8)
            ot = opool.tile([P, 4, D], F32, name="ot")
            nc.vector.tensor_tensor(
                out=ot[:],
                in0=v_tiles[u][:].rearrange("p (b d) -> p b d", b=4),
                in1=xn[q][:, :, m, :],
                op=ALU.add,
            )
            nc.sync.dma_start(
                out=out[4 * q : 4 * q + 4, P * m : P * m + P, :].rearrange("b c d -> c b d"),
                in_=ot[:],
            )

        state = {"mm2": 0, "res": 0, "qu": 0}

        def feed_mm2():
            while state["mm2"] < 32:
                u = state["mm2"]
                need = 2 * (u // 8) + (1 if u % 8 < 4 else 2)
                room = 3
                if u - state["res"] >= room or state["qu"] < need:
                    break
                mm2(u)
                state["mm2"] = u + 1

        def do_resid(n):
            for i in range(n):
                resid(state["res"])
                state["res"] = state["res"] + 1
                feed_mm2()

        def do_quant_u(q, g):
            quant_u(q, g)
            state["qu"] = 2 * q + g + 1
            feed_mm2()

        square(0)
        chain_a(0)
        square(1)
        chain_a(1)
        place_ln()
        chain_s(0)
        chain_c(0)
        chain_s(1)
        square(2)
        square(3)
        chain_a(2)
        for s in range(-4, 18):
            if 0 <= s < B:
                hs2(s)
            if 0 <= s + 1 < B:
                mm1(s + 1)
            if 0 <= s < B:
                transp(s)
            first, second = RES_AT.get(s, (0, 0))
            do_resid(first)
            for k in range(len(GROUPS)):
                if CS.get(k) == s:
                    chain_s(k)
            if 0 <= s + 4 < B:
                ln_a(s + 4)
            if 0 <= s + 3 < B:
                ln_b(s + 3)
            do_resid(second)
            if 0 <= s + 2 < B:
                quant_h(s + 2)
            for k in range(len(GROUPS)):
                if CC.get(k) == s:
                    chain_c(k)
            if s >= 4 and (s - 4) % 4 == 0 and (s - 4) // 4 <= 3:
                do_quant_u((s - 4) // 4, 0)
                do_quant_u((s - 4) // 4, 1)
            for b in SQ.get(s, ()):
                square(b)
            for k in range(len(GROUPS)):
                if CA.get(k) == s:
                    chain_a(k)
            for b in GR.get(s, ()):
                g_route(b)
